import numpy as np
import ml_dtypes


def mxq(x, axis, fmt="e4m3"):
    dtype, down = {"e4m3": (ml_dtypes.float8_e4m3fn, 7), "e5m2": (ml_dtypes.float8_e5m2, 14)}[fmt]
    v = np.moveaxis(np.asarray(x, np.float32).astype(ml_dtypes.bfloat16).astype(np.float64), axis, -1)
    blocks = v.reshape(v.shape[:-1] + (-1, 32))
    amax = np.abs(blocks).max(-1, keepdims=True)
    byte = np.maximum(np.where(amax > 0, np.frexp(amax)[1] - 1 + 127, 0) - down, 1)
    scale = np.exp2(byte - 127.0)
    codes = (blocks / scale).astype(np.float32).astype(dtype).astype(np.float64)
    return np.moveaxis((codes * scale).reshape(v.shape), -1, axis)


WIDE = False


def mx_kscale(k):
    if not WIDE:
        return np.ones(k)
    levels = np.array([10, -10, 5, -5, 0])
    a = np.random.permutation(np.resize(levels, k // 512 * 4)).reshape(k // 512, 4)
    idx = np.arange(k)
    return np.exp2(a[idx // 512, idx % 128 // 32])


BF16 = ml_dtypes.bfloat16


def bf(x):
    return np.asarray(x, np.float32).astype(BF16)


def f64(x):
    return np.asarray(x).astype(np.float64)


N, IN, HID, OUT, MLP, NF = 128, 256, 512, 512, 512, 8
FS = N // NF
G = 3 * HID


def sigmoid(v):
    return 1.0 / (1.0 + np.exp(-v))


def draw_hiddens():
    amp = 0.2 + 0.8 * np.random.random((N, 1))
    centre = np.repeat(np.random.standard_normal((NF, HID)), FS, axis=0)
    return amp * np.random.standard_normal((N, HID)) + 0.3 * centre


def setup_inputs():
    s = mx_kscale(OUT)
    return {
        "ag_diff": bf(np.random.standard_normal((N, OUT)) * 2.0 * s),
        "tension": bf(2.5 + 3.5 * np.random.random((N, 1))),
        "hiddens": bf(draw_hiddens()),
        "W_io": bf(np.random.standard_normal((G, OUT)) * 0.4 / np.sqrt(OUT) / s),
        "w_it": bf(np.random.standard_normal(G) * 0.1),
        "W_hh": bf(np.random.standard_normal((G, HID)) / np.sqrt(HID)),
        "b_ih": bf(np.random.standard_normal(G) * 0.1),
        "b_hh": bf(np.random.standard_normal(G) * 0.1),
    }


def reference(ag_diff, tension, hiddens, W_io, w_it, W_hh, b_ih, b_hh):
    h = f64(hiddens)
    gi = (mxq(f64(ag_diff), 1, "e4m3") @ mxq(f64(W_io), 1, "e4m3").T) + f64(tension) * f64(w_it) + f64(b_ih)
    gh = (mxq(h, 1, "e4m3") @ mxq(f64(W_hh), 1, "e4m3").T) + f64(b_hh)
    i_r, i_z, i_n = np.split(gi, 3, axis=-1)
    h_r, h_z, h_n = np.split(gh, 3, axis=-1)
    r = sigmoid(i_r + h_r)
    z = sigmoid(i_z + h_z)
    n = np.tanh(i_n + r * h_n)
    new_h = (1.0 - z) * n + z * h
    nh = new_h.reshape(NF, FS, HID)
    fmean = nh.mean(axis=1, keepdims=True)
    return (0.85 * nh + 0.15 * fmean).reshape(N, HID)

@@ -1,0 +1,255 @@
+from contextlib import ExitStack
+
+import concourse.mybir as mybir
+from concourse.masks import make_identity
+
+F32 = mybir.dt.float32
+BF16 = mybir.dt.bfloat16
+U32 = mybir.dt.uint32
+U8 = mybir.dt.uint8
+FP8X4 = mybir.dt.float8_e4m3fn_x4
+ADD = mybir.AluOpType.add
+MULT = mybir.AluOpType.mult
+ACT = mybir.ActivationFunctionType
+
+P = 128
+CELLS = 128
+K = 512
+HID = 512
+WORDS = K // 2
+BLOCKS_PER_GATE = HID // P
+GATE_R, GATE_Z, GATE_N = 0, 1, 2
+GATE_ORDER = (GATE_R, GATE_N, GATE_Z)
+N_BLOCKS = 3 * BLOCKS_PER_GATE
+PAIR = 2
+PAIRS = BLOCKS_PER_GATE // PAIR
+FACTION = 16
+KEEP = 0.85
+MEAN_OVER_KEPT = (1.0 - KEEP) / (FACTION * KEEP)
+TENSION_ROW = 3 * N_BLOCKS
+
+FLOPS = 2 * 2 * CELLS * K * 3 * HID
+
+
+def tile_phiaslossengine_pb_s_kernel(tc, ag_diff, tension, hiddens, W_io, w_it, W_hh, b_ih, b_hh, out):
+    nc = tc.nc
+    with ExitStack() as stack:
+        keep = stack.enter_context(tc.tile_pool(name="keep", bufs=1))
+        flip_pool = stack.enter_context(tc.psum_pool(name="flip", bufs=4))
+        acc_pool = stack.enter_context(tc.psum_pool(name="acc", bufs=4))
+        stack.enter_context(tc.manual_schedule())
+
+        def pair_tile(name, pair):
+            return keep.tile([P, PAIR, CELLS], F32, name="%s_%d" % (name, pair))
+
+        vecs = keep.tile([P, P], BF16, name="vecs")
+        nc.gpsimd.memset(vecs[:], 0.0)
+        ag_sb = keep.tile([P, K], BF16, name="ag_sb")
+        nc.sync.dma_start(out=ag_sb[:], in_=ag_diff)
+        h_sb = keep.tile([P, K], BF16, name="h_sb")
+        nc.sync.dma_start(out=h_sb[:], in_=hiddens)
+        for v, vec in enumerate((w_it, b_ih, b_hh)):
+            nc.scalar.dma_start(out=vecs[v * N_BLOCKS : (v + 1) * N_BLOCKS, :], in_=vec.rearrange("(b p) -> b p", p=P))
+        nc.scalar.dma_start(out=vecs[TENSION_ROW : TENSION_ROW + 1, :], in_=tension.rearrange("c o -> o c"))
+        w_sb = {}
+        for gate in GATE_ORDER:
+            for m, w_dram in enumerate((W_io, W_hh)):
+                w_tile = keep.tile([P, BLOCKS_PER_GATE * K], BF16, name="w_%d_%d" % (gate, m))
+                w_sb[(gate, m)] = w_tile
+                cuts = PAIRS if (gate, m) == (GATE_ORDER[-1], 1) else 1
+                blocks = BLOCKS_PER_GATE // cuts
+                for c in range(cuts):
+                    first = gate * BLOCKS_PER_GATE + c * blocks
+                    nc.sync.dma_start(
+                        out=w_tile[:, c * blocks * K : (c + 1) * blocks * K].rearrange("p (b k) -> p b k", b=blocks),
+                        in_=w_dram[first * P : (first + blocks) * P, :].rearrange("(b p) k -> p b k", p=P),
+                    )
+
+        warm = keep.tile([P, 1], F32, name="warm")
+        nc.vector.memset(warm[:], 0.0)
+        nc.scalar.activation(out=warm[:], in_=warm[:], func=ACT.Sigmoid)
+
+        ident_f32 = keep.tile([P, P], F32, name="ident_f32")
+        make_identity(nc, ident_f32[:])
+        ident_bf16 = keep.tile([P, P], BF16, name="ident_bf16")
+        nc.vector.tensor_copy(out=ident_bf16[:], in_=ident_f32[:])
+
+        def flip_pair(first_words, second_words, name):
+            bank = flip_pool.tile([P, PAIR, 2, P], F32, tag="flip")
+            for b, words in enumerate((first_words, second_words)):
+                for u in range(2):
+                    nc.tensor.transpose(bank[:, b, u, :], words[:, u * P : (u + 1) * P], ident_f32[:])
+            grouped = keep.tile([P, PAIR * P * 4], BF16, name="grouped_" + name, align_bytes=64)
+            nc.scalar.copy(
+                out=grouped[:].bitcast(F32).rearrange("p (b c u) -> p b c u", b=PAIR, u=2),
+                in_=bank[:].rearrange("p b u c -> p b c u"),
+            )
+            return grouped
+
+        def quantise(grouped, name):
+            codes = keep.tile([P, PAIR * P], U32, name="codes_" + name, align_bytes=64)
+            scales = keep.tile([P, PAIR * P], U8, name="scales_" + name, align_bytes=64)
+            nc.vector.quantize_mx(out=codes[:].bitcast(FP8X4), scales=scales[:], in_=grouped[:])
+            return codes, scales
+
+        grouped_x = flip_pair(ag_sb[:].bitcast(F32), h_sb[:].bitcast(F32), "x")
+        hT_ps = flip_pool.tile([P, BLOCKS_PER_GATE, CELLS], BF16, tag="flip")
+        for blk in range(BLOCKS_PER_GATE):
+            nc.tensor.transpose(hT_ps[:, blk, :], h_sb[:, blk * P : (blk + 1) * P], ident_bf16[:])
+        h_kept = keep.tile([P, BLOCKS_PER_GATE, CELLS], F32, name="h_kept")
+        nc.scalar.activation(out=h_kept[:], in_=hT_ps[:], func=ACT.Copy, scale=KEEP)
+
+        vecs_ps = flip_pool.tile([P, P], BF16, tag="flip")
+        nc.tensor.transpose(vecs_ps[:], vecs[:], ident_bf16[:])
+        tension_ps = flip_pool.tile([P, CELLS], F32, tag="flip")
+        nc.tensor.matmul(
+            out=tension_ps[:],
+            lhsT=ident_bf16[:, TENSION_ROW : TENSION_ROW + 1].to_broadcast([P, P]),
+            rhs=vecs[:],
+            start=True,
+            stop=True,
+        )
+        cols = keep.tile([P, 3 * N_BLOCKS], F32, name="cols")
+        nc.vector.tensor_copy(out=cols[:], in_=vecs_ps[:, 0 : 3 * N_BLOCKS])
+        w_it_col = cols[:, 0:N_BLOCKS]
+        b_ih_col = cols[:, N_BLOCKS : 2 * N_BLOCKS]
+        b_hh_col = cols[:, 2 * N_BLOCKS : 3 * N_BLOCKS]
+        b_sum_col = keep.tile([P, N_BLOCKS], F32, name="b_sum_col")
+        nc.vector.tensor_add(out=b_sum_col[:], in0=b_ih_col, in1=b_hh_col)
+        tension_rows = keep.tile([P, CELLS], F32, name="tension_rows")
+        nc.vector.tensor_copy(out=tension_rows[:], in_=tension_ps[:])
+
+        side = keep.tile([P, N_BLOCKS, CELLS], F32, name="side")
+        for gate in GATE_ORDER:
+            bias_col = b_ih_col if gate == GATE_N else b_sum_col[:]
+            for blk in range(gate * BLOCKS_PER_GATE, (gate + 1) * BLOCKS_PER_GATE):
+                nc.vector.tensor_scalar(
+                    out=side[:, blk, :],
+                    in0=tension_rows[:],
+                    scalar1=w_it_col[:, blk : blk + 1],
+                    scalar2=bias_col[:, blk : blk + 1],
+                    op0=MULT,
+                    op1=ADD,
+                )
+        codes_x, scales_x = quantise(grouped_x, "x")
+
+        units = [(gate, m, pair) for gate in GATE_ORDER for m in range(2) for pair in range(PAIRS)]
+        grouped_w = {}
+        quantised_w = {}
+        acc = {}
+        gate_out = {}
+        diff = {}
+        blend = {}
+
+        def flip_weights(gate, m, pair):
+            words = w_sb[(gate, m)][:].bitcast(F32)
+            first = pair * PAIR * WORDS
+            grouped_w[(gate, m, pair)] = flip_pair(
+                words[:, first : first + WORDS], words[:, first + WORDS : first + 2 * WORDS], "%d_%d_%d" % (gate, m, pair)
+            )
+
+        def quantise_weights(gate, m, pair):
+            quantised_w[(gate, m, pair)] = quantise(grouped_w[(gate, m, pair)], "%d_%d_%d" % (gate, m, pair))
+
+        def mx_pass(acc_block, gate, m, pair, b, start, stop):
+            codes, scales = quantised_w[(gate, m, pair)]
+            w_cols = slice(b * P, (b + 1) * P)
+            x_cols = slice(m * CELLS, (m + 1) * CELLS)
+            nc.tensor.matmul_mx(
+                out=acc_block,
+                lhsT=codes[:, w_cols].bitcast(FP8X4),
+                lhsT_scale=scales[:, w_cols],
+                rhs=codes_x[:, x_cols].bitcast(FP8X4),
+                rhs_scale=scales_x[:, x_cols],
+                start=start,
+                stop=stop,
+            )
+
+        def multiply(gate, m, pair):
+            if m == 0:
+                return
+            if gate == GATE_N:
+                for mm in range(2):
+                    acc_m = acc_pool.tile([P, PAIR, CELLS], F32, tag="acc")
+                    for b in range(PAIR):
+                        mx_pass(acc_m[:, b, :], gate, mm, pair, b, True, True)
+                    acc[(gate, pair, mm)] = acc_m
+            else:
+                acc_sum = acc_pool.tile([P, PAIR, CELLS], F32, tag="acc")
+                for b in range(PAIR):
+                    mx_pass(acc_sum[:, b, :], gate, 0, pair, b, True, False)
+                    mx_pass(acc_sum[:, b, :], gate, 1, pair, b, False, True)
+                acc[(gate, pair, 0)] = acc_sum
+
+        def gate_function(gate, m, pair):
+            if m == 0:
+                return
+            blk = gate * BLOCKS_PER_GATE + pair * PAIR
+            pre = pair_tile("pre%d" % gate, pair)
+            nc.vector.tensor_add(out=pre[:], in0=acc[(gate, pair, 0)][:], in1=side[:, blk : blk + PAIR, :])
+            if gate == GATE_N:
+                rh = pair_tile("rh", pair)
+                for b in range(PAIR):
+                    nc.vector.scalar_tensor_tensor(
+                        out=rh[:, b, :],
+                        in0=acc[(gate, pair, 1)][:, b, :],
+                        scalar=b_hh_col[:, blk + b : blk + b + 1],
+                        in1=gate_out[(GATE_R, pair)][:, b, :],
+                        op0=ADD,
+                        op1=MULT,
+                    )
+                nc.vector.tensor_add(out=pre[:], in0=pre[:], in1=rh[:])
+            result = pair_tile("gate%d" % gate, pair)
+            nc.scalar.activation(out=result[:], in_=pre[:], func=ACT.Tanh if gate == GATE_N else ACT.Sigmoid)
+            gate_out[(gate, pair)] = result
+
+        def after_function(gate, m, pair):
+            if m == 0:
+                return
+            if gate == GATE_N:
+                diff[pair] = pair_tile("diff", pair)
+                nc.vector.scalar_tensor_tensor(
+                    out=diff[pair][:],
+                    in0=gate_out[(GATE_N, pair)][:],
+                    scalar=-KEEP,
+                    in1=h_kept[:, pair * PAIR : (pair + 1) * PAIR, :],
+                    op0=MULT,
+                    op1=ADD,
+                )
+            if gate == GATE_Z:
+                kept = pair_tile("kept", pair)
+                nc.vector.tensor_mul(out=kept[:], in0=gate_out[(GATE_Z, pair)][:], in1=diff[pair][:])
+                nc.vector.scalar_tensor_tensor(
+                    out=kept[:], in0=gate_out[(GATE_N, pair)][:], scalar=KEEP, in1=kept[:], op0=MULT, op1=ADD
+                )
+                by_faction = "p b (f s) -> p (b f) s"
+                n_sums = PAIR * CELLS // FACTION
+                sums = keep.tile([P, n_sums], F32, name="sums_%d" % pair)
+                nc.vector.tensor_reduce(
+                    out=sums[:], in_=kept[:].rearrange(by_faction, s=FACTION), axis=mybir.AxisListType.X, op=ADD
+                )
+                blend[pair] = pair_tile("blend", pair)
+                nc.vector.scalar_tensor_tensor(
+                    out=blend[pair][:].rearrange(by_faction, s=FACTION),
+                    in0=sums[:].unsqueeze(2).to_broadcast([P, n_sums, FACTION]),
+                    scalar=MEAN_OVER_KEPT,
+                    in1=kept[:].rearrange(by_faction, s=FACTION),
+                    op0=MULT,
+                    op1=ADD,
+                )
+
+        def store(gate, m, pair):
+            if m == 0 or gate != GATE_Z:
+                return
+            out_ps = acc_pool.tile([P, PAIR, P], F32, tag="acc")
+            for b in range(PAIR):
+                nc.tensor.transpose(out_ps[:, b, :], blend[pair][:, b, :], ident_f32[:])
+            out_sb = pair_tile("out_sb", pair)
+            nc.scalar.copy(out=out_sb[:], in_=out_ps[:])
+            nc.sync.dma_start(out=out[:, pair * PAIR * P : (pair + 1) * PAIR * P], in_=out_sb[:].rearrange("p b h -> p (b h)"))
+
+        stages = (flip_weights, quantise_weights, multiply, gate_function, after_function, store)
+        for tick in range(len(units) + len(stages) - 1):
+            for lag, stage in enumerate(stages):
+                if 0 <= tick - lag < len(units):
+                    stage(*units[tick - lag])

@@ -37,7 +37,6 @@ def tile_phiaslossengine_pb_s_kernel(tc, ag_diff, tension, hiddens, W_io, w_it, 
         keep = stack.enter_context(tc.tile_pool(name="keep", bufs=1))
         flip_pool = stack.enter_context(tc.psum_pool(name="flip", bufs=4))
         acc_pool = stack.enter_context(tc.psum_pool(name="acc", bufs=4))
-        stack.enter_context(tc.manual_schedule())
 
         def pair_tile(name, pair):
             return keep.tile([P, PAIR, CELLS], F32, name="%s_%d" % (name, pair))
@@ -49,8 +48,8 @@ def tile_phiaslossengine_pb_s_kernel(tc, ag_diff, tension, hiddens, W_io, w_it, 
         h_sb = keep.tile([P, K], BF16, name="h_sb")
         nc.sync.dma_start(out=h_sb[:], in_=hiddens)
         for v, vec in enumerate((w_it, b_ih, b_hh)):
-            nc.scalar.dma_start(out=vecs[v * N_BLOCKS : (v + 1) * N_BLOCKS, :], in_=vec.rearrange("(b p) -> b p", p=P))
-        nc.scalar.dma_start(out=vecs[TENSION_ROW : TENSION_ROW + 1, :], in_=tension.rearrange("c o -> o c"))
+            nc.sync.dma_start(out=vecs[v * N_BLOCKS : (v + 1) * N_BLOCKS, :], in_=vec.rearrange("(b p) -> b p", p=P))
+        nc.sync.dma_start(out=vecs[TENSION_ROW : TENSION_ROW + 1, :], in_=tension.rearrange("c o -> o c"))
         w_sb = {}
         for gate in GATE_ORDER:
             for m, w_dram in enumerate((W_io, W_hh)):

@@ -38,8 +38,8 @@ def tile_phiaslossengine_pb_s_kernel(tc, ag_diff, tension, hiddens, W_io, w_it, 
         flip_pool = stack.enter_context(tc.psum_pool(name="flip", bufs=4))
         acc_pool = stack.enter_context(tc.psum_pool(name="acc", bufs=4))
 
-        def pair_tile(name, pair):
-            return keep.tile([P, PAIR, CELLS], F32, name="%s_%d" % (name, pair))
+        def block_tile(name, j):
+            return keep.tile([P, CELLS], F32, name="%s_%d" % (name, j))
 
         vecs = keep.tile([P, P], BF16, name="vecs")
         nc.gpsimd.memset(vecs[:], 0.0)
@@ -132,7 +132,7 @@ def tile_phiaslossengine_pb_s_kernel(tc, ag_diff, tension, hiddens, W_io, w_it, 
                 )
         codes_x, scales_x = quantise(grouped_x, "x")
 
-        units = [(gate, m, pair) for gate in GATE_ORDER for m in range(2) for pair in range(PAIRS)]
+        units = [(j, gate) for gate in GATE_ORDER for j in range(BLOCKS_PER_GATE)]
         grouped_w = {}
         quantised_w = {}
         acc = {}
@@ -140,112 +140,87 @@ def tile_phiaslossengine_pb_s_kernel(tc, ag_diff, tension, hiddens, W_io, w_it, 
         diff = {}
         blend = {}
 
-        def flip_weights(gate, m, pair):
-            words = w_sb[(gate, m)][:].bitcast(F32)
-            first = pair * PAIR * WORDS
-            grouped_w[(gate, m, pair)] = flip_pair(
-                words[:, first : first + WORDS], words[:, first + WORDS : first + 2 * WORDS], "%d_%d_%d" % (gate, m, pair)
+        def flip_weights(j, gate):
+            grouped_w[(j, gate)] = flip_pair(
+                w_sb[(gate, 0)][:].bitcast(F32)[:, j * WORDS : (j + 1) * WORDS],
+                w_sb[(gate, 1)][:].bitcast(F32)[:, j * WORDS : (j + 1) * WORDS],
+                "%d_%d" % (j, gate),
             )
 
-        def quantise_weights(gate, m, pair):
-            quantised_w[(gate, m, pair)] = quantise(grouped_w[(gate, m, pair)], "%d_%d_%d" % (gate, m, pair))
+        def quantise_weights(j, gate):
+            quantised_w[(j, gate)] = quantise(grouped_w[(j, gate)], "%d_%d" % (j, gate))
 
-        def mx_pass(acc_block, gate, m, pair, b, start, stop):
-            codes, scales = quantised_w[(gate, m, pair)]
-            w_cols = slice(b * P, (b + 1) * P)
-            x_cols = slice(m * CELLS, (m + 1) * CELLS)
-            nc.tensor.matmul_mx(
-                out=acc_block,
-                lhsT=codes[:, w_cols].bitcast(FP8X4),
-                lhsT_scale=scales[:, w_cols],
-                rhs=codes_x[:, x_cols].bitcast(FP8X4),
-                rhs_scale=scales_x[:, x_cols],
-                start=start,
-                stop=stop,
-            )
+        def multiply(j, gate):
+            codes, scales = quantised_w[(j, gate)]
+            apart = gate == GATE_N
+            products = acc_pool.tile([P, 2, CELLS], F32, tag="acc")
+            for m in range(2):
+                cols_m = slice(m * P, (m + 1) * P)
+                nc.tensor.matmul_mx(
+                    out=products[:, m if apart else 0, :],
+                    lhsT=codes[:, cols_m].bitcast(FP8X4),
+                    lhsT_scale=scales[:, cols_m],
+                    rhs=codes_x[:, cols_m].bitcast(FP8X4),
+                    rhs_scale=scales_x[:, cols_m],
+                    start=apart or m == 0,
+                    stop=apart or m == 1,
+                )
+            acc[(j, gate)] = products
 
-        def multiply(gate, m, pair):
-            if m == 0:
-                return
+        def gate_function(j, gate):
+            blk = gate * BLOCKS_PER_GATE + j
+            pre = block_tile("pre%d" % gate, j)
+            nc.vector.tensor_add(out=pre[:], in0=acc[(j, gate)][:, 0, :], in1=side[:, blk, :])
             if gate == GATE_N:
-                for mm in range(2):
-                    acc_m = acc_pool.tile([P, PAIR, CELLS], F32, tag="acc")
-                    for b in range(PAIR):
-                        mx_pass(acc_m[:, b, :], gate, mm, pair, b, True, True)
-                    acc[(gate, pair, mm)] = acc_m
-            else:
-                acc_sum = acc_pool.tile([P, PAIR, CELLS], F32, tag="acc")
-                for b in range(PAIR):
-                    mx_pass(acc_sum[:, b, :], gate, 0, pair, b, True, False)
-                    mx_pass(acc_sum[:, b, :], gate, 1, pair, b, False, True)
-                acc[(gate, pair, 0)] = acc_sum
-
-        def gate_function(gate, m, pair):
-            if m == 0:
-                return
-            blk = gate * BLOCKS_PER_GATE + pair * PAIR
-            pre = pair_tile("pre%d" % gate, pair)
-            nc.vector.tensor_add(out=pre[:], in0=acc[(gate, pair, 0)][:], in1=side[:, blk : blk + PAIR, :])
-            if gate == GATE_N:
-                rh = pair_tile("rh", pair)
-                for b in range(PAIR):
-                    nc.vector.scalar_tensor_tensor(
-                        out=rh[:, b, :],
-                        in0=acc[(gate, pair, 1)][:, b, :],
-                        scalar=b_hh_col[:, blk + b : blk + b + 1],
-                        in1=gate_out[(GATE_R, pair)][:, b, :],
-                        op0=ADD,
-                        op1=MULT,
-                    )
-                nc.vector.tensor_add(out=pre[:], in0=pre[:], in1=rh[:])
-            result = pair_tile("gate%d" % gate, pair)
-            nc.scalar.activation(out=result[:], in_=pre[:], func=ACT.Tanh if gate == GATE_N else ACT.Sigmoid)
-            gate_out[(gate, pair)] = result
-
-        def after_function(gate, m, pair):
-            if m == 0:
-                return
-            if gate == GATE_N:
-                diff[pair] = pair_tile("diff", pair)
+                rh = block_tile("rh", j)
                 nc.vector.scalar_tensor_tensor(
-                    out=diff[pair][:],
-                    in0=gate_out[(GATE_N, pair)][:],
-                    scalar=-KEEP,
-                    in1=h_kept[:, pair * PAIR : (pair + 1) * PAIR, :],
-                    op0=MULT,
-                    op1=ADD,
+                    out=rh[:],
+                    in0=acc[(j, gate)][:, 1, :],
+                    scalar=b_hh_col[:, blk : blk + 1],
+                    in1=gate_out[(j, GATE_R)][:],
+                    op0=ADD,
+                    op1=MULT,
+                )
+                nc.vector.tensor_add(out=pre[:], in0=pre[:], in1=rh[:])
+            result = block_tile("gate%d" % gate, j)
+            nc.scalar.activation(out=result[:], in_=pre[:], func=ACT.Tanh if gate == GATE_N else ACT.Sigmoid)
+            gate_out[(j, gate)] = result
+
+        def after_function(j, gate):
+            if gate == GATE_N:
+                diff[j] = block_tile("diff", j)
+                nc.vector.scalar_tensor_tensor(
+                    out=diff[j][:], in0=gate_out[(j, GATE_N)][:], scalar=-KEEP, in1=h_kept[:, j, :], op0=MULT, op1=ADD
                 )
             if gate == GATE_Z:
-                kept = pair_tile("kept", pair)
-                nc.vector.tensor_mul(out=kept[:], in0=gate_out[(GATE_Z, pair)][:], in1=diff[pair][:])
+                kept = block_tile("kept", j)
+                nc.vector.tensor_mul(out=kept[:], in0=gate_out[(j, GATE_Z)][:], in1=diff[j][:])
                 nc.vector.scalar_tensor_tensor(
-                    out=kept[:], in0=gate_out[(GATE_N, pair)][:], scalar=KEEP, in1=kept[:], op0=MULT, op1=ADD
+                    out=kept[:], in0=gate_out[(j, GATE_N)][:], scalar=KEEP, in1=kept[:], op0=MULT, op1=ADD
                 )
-                by_faction = "p b (f s) -> p (b f) s"
-                n_sums = PAIR * CELLS // FACTION
-                sums = keep.tile([P, n_sums], F32, name="sums_%d" % pair)
+                by_faction = "p (f s) -> p f s"
+                factions = CELLS // FACTION
+                sums = keep.tile([P, factions], F32, name="sums_%d" % j)
                 nc.vector.tensor_reduce(
                     out=sums[:], in_=kept[:].rearrange(by_faction, s=FACTION), axis=mybir.AxisListType.X, op=ADD
                 )
-                blend[pair] = pair_tile("blend", pair)
+                blend[j] = block_tile("blend", j)
                 nc.vector.scalar_tensor_tensor(
-                    out=blend[pair][:].rearrange(by_faction, s=FACTION),
-                    in0=sums[:].unsqueeze(2).to_broadcast([P, n_sums, FACTION]),
+                    out=blend[j][:].rearrange(by_faction, s=FACTION),
+                    in0=sums[:].unsqueeze(2).to_broadcast([P, factions, FACTION]),
                     scalar=MEAN_OVER_KEPT,
                     in1=kept[:].rearrange(by_faction, s=FACTION),
                     op0=MULT,
                     op1=ADD,
                 )
 
-        def store(gate, m, pair):
-            if m == 0 or gate != GATE_Z:
-                return
-            out_ps = acc_pool.tile([P, PAIR, P], F32, tag="acc")
-            for b in range(PAIR):
-                nc.tensor.transpose(out_ps[:, b, :], blend[pair][:, b, :], ident_f32[:])
-            out_sb = pair_tile("out_sb", pair)
-            nc.scalar.copy(out=out_sb[:], in_=out_ps[:])
-            nc.sync.dma_start(out=out[:, pair * PAIR * P : (pair + 1) * PAIR * P], in_=out_sb[:].rearrange("p b h -> p (b h)"))
+        def store(j, gate):
+            if gate == GATE_Z:
+                out_ps = acc_pool.tile([P, P], F32, tag="acc")
+                nc.tensor.transpose(out_ps[:], blend[j][:], ident_f32[:])
+                out_sb = block_tile("out_sb", j)
+                nc.scalar.copy(out=out_sb[:], in_=out_ps[:])
+                nc.sync.dma_start(out=out[:, j * P : (j + 1) * P], in_=out_sb[:])
 
         stages = (flip_weights, quantise_weights, multiply, gate_function, after_function, store)
         for tick in range(len(units) + len(stages) - 1):

@@ -38,8 +38,8 @@ def tile_phiaslossengine_pb_s_kernel(tc, ag_diff, tension, hiddens, W_io, w_it, 
         flip_pool = stack.enter_context(tc.psum_pool(name="flip", bufs=4))
         acc_pool = stack.enter_context(tc.psum_pool(name="acc", bufs=4))
 
-        def block_tile(name, j):
-            return keep.tile([P, CELLS], F32, name="%s_%d" % (name, j))
+        def pair_tile(name, pair):
+            return keep.tile([P, PAIR, CELLS], F32, name="%s_%d" % (name, pair))
 
         vecs = keep.tile([P, P], BF16, name="vecs")
         nc.gpsimd.memset(vecs[:], 0.0)
@@ -132,7 +132,7 @@ def tile_phiaslossengine_pb_s_kernel(tc, ag_diff, tension, hiddens, W_io, w_it, 
                 )
         codes_x, scales_x = quantise(grouped_x, "x")
 
-        units = [(j, gate) for gate in GATE_ORDER for j in range(BLOCKS_PER_GATE)]
+        units = [(gate, m, pair) for gate in GATE_ORDER for m in range(2) for pair in range(PAIRS)]
         grouped_w = {}
         quantised_w = {}
         acc = {}
@@ -140,90 +140,131 @@ def tile_phiaslossengine_pb_s_kernel(tc, ag_diff, tension, hiddens, W_io, w_it, 
         diff = {}
         blend = {}
 
-        def flip_weights(j, gate):
-            grouped_w[(j, gate)] = flip_pair(
-                w_sb[(gate, 0)][:].bitcast(F32)[:, j * WORDS : (j + 1) * WORDS],
-                w_sb[(gate, 1)][:].bitcast(F32)[:, j * WORDS : (j + 1) * WORDS],
-                "%d_%d" % (j, gate),
+        def flip_weights(gate, m, pair):
+            words = w_sb[(gate, m)][:].bitcast(F32)
+            first = pair * PAIR * WORDS
+            grouped_w[(gate, m, pair)] = flip_pair(
+                words[:, first : first + WORDS], words[:, first + WORDS : first + 2 * WORDS], "%d_%d_%d" % (gate, m, pair)
             )
 
-        def quantise_weights(j, gate):
-            quantised_w[(j, gate)] = quantise(grouped_w[(j, gate)], "%d_%d" % (j, gate))
+        def quantise_weights(gate, m, pair):
+            quantised_w[(gate, m, pair)] = quantise(grouped_w[(gate, m, pair)], "%d_%d_%d" % (gate, m, pair))
 
-        def multiply(j, gate):
-            codes, scales = quantised_w[(j, gate)]
-            apart = gate == GATE_N
-            products = acc_pool.tile([P, 2, CELLS], F32, tag="acc")
-            for m in range(2):
-                cols_m = slice(m * P, (m + 1) * P)
-                nc.tensor.matmul_mx(
-                    out=products[:, m if apart else 0, :],
-                    lhsT=codes[:, cols_m].bitcast(FP8X4),
-                    lhsT_scale=scales[:, cols_m],
-                    rhs=codes_x[:, cols_m].bitcast(FP8X4),
-                    rhs_scale=scales_x[:, cols_m],
-                    start=apart or m == 0,
-                    stop=apart or m == 1,
-                )
-            acc[(j, gate)] = products
+        def mx_pass(acc_block, gate, m, blk, start, stop):
+            codes, scales = quantised_w[(gate, m, blk // PAIR)]
+            w_cols = slice((blk % PAIR) * P, (blk % PAIR + 1) * P)
+            x_cols = slice(m * CELLS, (m + 1) * CELLS)
+            nc.tensor.matmul_mx(
+                out=acc_block,
+                lhsT=codes[:, w_cols].bitcast(FP8X4),
+                lhsT_scale=scales[:, w_cols],
+                rhs=codes_x[:, x_cols].bitcast(FP8X4),
+                rhs_scale=scales_x[:, x_cols],
+                start=start,
+                stop=stop,
+            )
 
-        def gate_function(j, gate):
-            blk = gate * BLOCKS_PER_GATE + j
-            pre = block_tile("pre%d" % gate, j)
-            nc.vector.tensor_add(out=pre[:], in0=acc[(j, gate)][:, 0, :], in1=side[:, blk, :])
+        def multiply(gate):
             if gate == GATE_N:
-                rh = block_tile("rh", j)
-                nc.vector.scalar_tensor_tensor(
-                    out=rh[:],
-                    in0=acc[(j, gate)][:, 1, :],
-                    scalar=b_hh_col[:, blk : blk + 1],
-                    in1=gate_out[(j, GATE_R)][:],
-                    op0=ADD,
-                    op1=MULT,
-                )
-                nc.vector.tensor_add(out=pre[:], in0=pre[:], in1=rh[:])
-            result = block_tile("gate%d" % gate, j)
-            nc.scalar.activation(out=result[:], in_=pre[:], func=ACT.Tanh if gate == GATE_N else ACT.Sigmoid)
-            gate_out[(j, gate)] = result
+                for m in range(2):
+                    acc_m = acc_pool.tile([P, BLOCKS_PER_GATE, CELLS], F32, tag="acc")
+                    for blk in range(BLOCKS_PER_GATE):
+                        mx_pass(acc_m[:, blk, :], gate, m, blk, True, True)
+                    acc[(gate, m)] = acc_m
+            else:
+                acc_sum = acc_pool.tile([P, BLOCKS_PER_GATE, CELLS], F32, tag="acc")
+                for blk in range(BLOCKS_PER_GATE):
+                    mx_pass(acc_sum[:, blk, :], gate, 0, blk, True, False)
+                    mx_pass(acc_sum[:, blk, :], gate, 1, blk, False, True)
+                acc[(gate, 0)] = acc_sum
 
-        def after_function(j, gate):
+        def blocks_of(pair):
+            return slice(pair * PAIR, (pair + 1) * PAIR)
+
+        def gate_function(gate):
+            first = gate * BLOCKS_PER_GATE
+            pre = [pair_tile("pre%d" % gate, pair) for pair in range(PAIRS)]
+            for pair in range(PAIRS):
+                nc.vector.tensor_add(
+                    out=pre[pair][:],
+                    in0=acc[(gate, 0)][:, blocks_of(pair), :],
+                    in1=side[:, first + pair * PAIR : first + (pair + 1) * PAIR, :],
+                )
             if gate == GATE_N:
-                diff[j] = block_tile("diff", j)
-                nc.vector.scalar_tensor_tensor(
-                    out=diff[j][:], in0=gate_out[(j, GATE_N)][:], scalar=-KEEP, in1=h_kept[:, j, :], op0=MULT, op1=ADD
-                )
-            if gate == GATE_Z:
-                kept = block_tile("kept", j)
-                nc.vector.tensor_mul(out=kept[:], in0=gate_out[(j, GATE_Z)][:], in1=diff[j][:])
-                nc.vector.scalar_tensor_tensor(
-                    out=kept[:], in0=gate_out[(j, GATE_N)][:], scalar=KEEP, in1=kept[:], op0=MULT, op1=ADD
-                )
-                by_faction = "p (f s) -> p f s"
-                factions = CELLS // FACTION
-                sums = keep.tile([P, factions], F32, name="sums_%d" % j)
-                nc.vector.tensor_reduce(
-                    out=sums[:], in_=kept[:].rearrange(by_faction, s=FACTION), axis=mybir.AxisListType.X, op=ADD
-                )
-                blend[j] = block_tile("blend", j)
-                nc.vector.scalar_tensor_tensor(
-                    out=blend[j][:].rearrange(by_faction, s=FACTION),
-                    in0=sums[:].unsqueeze(2).to_broadcast([P, factions, FACTION]),
-                    scalar=MEAN_OVER_KEPT,
-                    in1=kept[:].rearrange(by_faction, s=FACTION),
-                    op0=MULT,
-                    op1=ADD,
-                )
+                rh = [pair_tile("rh", pair) for pair in range(PAIRS)]
+                for blk in range(BLOCKS_PER_GATE):
+                    nc.vector.scalar_tensor_tensor(
+                        out=rh[blk // PAIR][:, blk % PAIR, :],
+                        in0=acc[(gate, 1)][:, blk, :],
+                        scalar=b_hh_col[:, first + blk : first + blk + 1],
+                        in1=gate_out[(GATE_R, blk // PAIR)][:, blk % PAIR, :],
+                        op0=ADD,
+                        op1=MULT,
+                    )
+                for pair in range(PAIRS):
+                    nc.vector.tensor_add(out=pre[pair][:], in0=pre[pair][:], in1=rh[pair][:])
+            for pair in range(PAIRS):
+                result = pair_tile("gate%d" % gate, pair)
+                nc.scalar.activation(out=result[:], in_=pre[pair][:], func=ACT.Tanh if gate == GATE_N else ACT.Sigmoid)
+                gate_out[(gate, pair)] = result
 
-        def store(j, gate):
+        def after_function(gate):
+            if gate == GATE_N:
+                for pair in range(PAIRS):
+                    diff[pair] = pair_tile("diff", pair)
+                    nc.vector.scalar_tensor_tensor(
+                        out=diff[pair][:],
+                        in0=gate_out[(GATE_N, pair)][:],
+                        scalar=-KEEP,
+                        in1=h_kept[:, blocks_of(pair), :],
+                        op0=MULT,
+                        op1=ADD,
+                    )
             if gate == GATE_Z:
-                out_ps = acc_pool.tile([P, P], F32, tag="acc")
-                nc.tensor.transpose(out_ps[:], blend[j][:], ident_f32[:])
-                out_sb = block_tile("out_sb", j)
+                by_faction = "p b (f s) -> p (b f) s"
+                n_sums = PAIR * CELLS // FACTION
+                moved = [pair_tile("moved", pair) for pair in range(PAIRS)]
+                kept = [pair_tile("kept", pair) for pair in range(PAIRS)]
+                sums = [keep.tile([P, n_sums], F32, name="sums_%d" % pair) for pair in range(PAIRS)]
+                for pair in range(PAIRS):
+                    nc.vector.tensor_mul(out=moved[pair][:], in0=gate_out[(GATE_Z, pair)][:], in1=diff[pair][:])
+                for pair in range(PAIRS):
+                    nc.vector.scalar_tensor_tensor(
+                        out=kept[pair][:], in0=gate_out[(GATE_N, pair)][:], scalar=KEEP, in1=moved[pair][:], op0=MULT, op1=ADD
+                    )
+                for pair in range(PAIRS):
+                    nc.vector.tensor_reduce(
+                        out=sums[pair][:], in_=kept[pair][:].rearrange(by_faction, s=FACTION), axis=mybir.AxisListType.X, op=ADD
+                    )
+                for pair in range(PAIRS):
+                    blend[pair] = pair_tile("blend", pair)
+                    nc.vector.scalar_tensor_tensor(
+                        out=blend[pair][:].rearrange(by_faction, s=FACTION),
+                        in0=sums[pair][:].unsqueeze(2).to_broadcast([P, n_sums, FACTION]),
+                        scalar=MEAN_OVER_KEPT,
+                        in1=kept[pair][:].rearrange(by_faction, s=FACTION),
+                        op0=MULT,
+                        op1=ADD,
+                    )
+
+        def store(gate):
+            if gate != GATE_Z:
+                return
+            for pair in range(PAIRS):
+                out_ps = acc_pool.tile([P, PAIR, P], F32, tag="acc")
+                for b in range(PAIR):
+                    nc.tensor.transpose(out_ps[:, b, :], blend[pair][:, b, :], ident_f32[:])
+                out_sb = pair_tile("out_sb", pair)
                 nc.scalar.copy(out=out_sb[:], in_=out_ps[:])
-                nc.sync.dma_start(out=out[:, j * P : (j + 1) * P], in_=out_sb[:])
+                nc.sync.dma_start(out=out[:, pair * PAIR * P : (pair + 1) * PAIR * P], in_=out_sb[:].rearrange("p b h -> p (b h)"))
 
-        stages = (flip_weights, quantise_weights, multiply, gate_function, after_function, store)
-        for tick in range(len(units) + len(stages) - 1):
-            for lag, stage in enumerate(stages):
+        unit_stages = (flip_weights, quantise_weights)
+        gate_stages = (multiply, gate_function, after_function, store)
+        for tick in range(len(units) + len(unit_stages) + len(gate_stages) - 1):
+            for lag, stage in enumerate(unit_stages):
                 if 0 <= tick - lag < len(units):
                     stage(*units[tick - lag])
+            for lag, stage in enumerate(gate_stages):
+                u = tick - len(unit_stages) - lag
+                if 0 <= u < len(units) and units[u][1:] == (1, PAIRS - 1):
+                    stage(units[u][0])

@@ -17,16 +17,16 @@ CELLS = 128
 K = 512
 HID = 512
 WORDS = K // 2
-BLOCKS_PER_GATE = HID // P
+E = 2
+HALVES = 2
+HALF = HID // HALVES
 GATE_R, GATE_Z, GATE_N = 0, 1, 2
 GATE_ORDER = (GATE_R, GATE_N, GATE_Z)
-N_BLOCKS = 3 * BLOCKS_PER_GATE
-PAIR = 2
-PAIRS = BLOCKS_PER_GATE // PAIR
 FACTION = 16
 KEEP = 0.85
 MEAN_OVER_KEPT = (1.0 - KEEP) / (FACTION * KEEP)
-TENSION_ROW = 3 * N_BLOCKS
+VEC_ROWS = 2
+VEC_HALVES = 3
 
 FLOPS = 2 * 2 * CELLS * K * 3 * HID
 
@@ -38,121 +38,107 @@ def tile_phiaslossengine_pb_s_kernel(tc, ag_diff, tension, hiddens, W_io, w_it, 
         flip_pool = stack.enter_context(tc.psum_pool(name="flip", bufs=4))
         acc_pool = stack.enter_context(tc.psum_pool(name="acc", bufs=4))
 
-        def pair_tile(name, pair):
-            return keep.tile([P, PAIR, CELLS], F32, name="%s_%d" % (name, pair))
+        def half_tile(name, half):
+            return keep.tile([P, E, CELLS], F32, name="%s_%d" % (name, half))
 
-        vecs = keep.tile([P, P], BF16, name="vecs")
-        nc.gpsimd.memset(vecs[:], 0.0)
+        vecs = keep.tile([P, VEC_HALVES * HALF], BF16, name="vecs")
+        nc.vector.memset(vecs[:], 0.0)
+        tens = keep.tile([P, CELLS], BF16, name="tens")
+        nc.vector.memset(tens[:], 0.0)
+        ones = keep.tile([P, P], BF16, name="ones")
+        nc.vector.memset(ones[:], 1.0)
+        warm = keep.tile([P, 1], F32, name="warm")
+        nc.vector.memset(warm[:], 0.0)
+        nc.scalar.activation(out=warm[:], in_=warm[:], func=ACT.Sigmoid)
+        ident = keep.tile([P, P], F32, name="ident")
+        make_identity(nc, ident[:])
+
         ag_sb = keep.tile([P, K], BF16, name="ag_sb")
         nc.sync.dma_start(out=ag_sb[:], in_=ag_diff)
         h_sb = keep.tile([P, K], BF16, name="h_sb")
         nc.sync.dma_start(out=h_sb[:], in_=hiddens)
-        for v, vec in enumerate((w_it, b_ih, b_hh)):
-            nc.sync.dma_start(out=vecs[v * N_BLOCKS : (v + 1) * N_BLOCKS, :], in_=vec.rearrange("(b p) -> b p", p=P))
-        nc.sync.dma_start(out=vecs[TENSION_ROW : TENSION_ROW + 1, :], in_=tension.rearrange("c o -> o c"))
+        units = [(half, gate, m) for half in range(HALVES) for gate in GATE_ORDER for m in range(2)]
         w_sb = {}
-        for gate in GATE_ORDER:
-            for m, w_dram in enumerate((W_io, W_hh)):
-                w_tile = keep.tile([P, BLOCKS_PER_GATE * K], BF16, name="w_%d_%d" % (gate, m))
-                w_sb[(gate, m)] = w_tile
-                cuts = PAIRS if (gate, m) == (GATE_ORDER[-1], 1) else 1
-                blocks = BLOCKS_PER_GATE // cuts
-                for c in range(cuts):
-                    first = gate * BLOCKS_PER_GATE + c * blocks
+        for i, unit in enumerate(units):
+            half, gate, m = unit
+            first = gate * HID + half * HALF
+            w_sb[unit] = keep.tile([P, E * K], BF16, name="w_%d_%d_%d" % unit)
+            nc.sync.dma_start(
+                out=w_sb[unit][:],
+                in_=(W_io, W_hh)[m][first : first + HALF, :].rearrange("(p e) k -> p (e k)", e=E),
+            )
+            if i == 1:
+                for v, vec in enumerate((w_it, b_ih, b_hh)):
                     nc.sync.dma_start(
-                        out=w_tile[:, c * blocks * K : (c + 1) * blocks * K].rearrange("p (b k) -> p b k", b=blocks),
-                        in_=w_dram[first * P : (first + blocks) * P, :].rearrange("(b p) k -> p b k", p=P),
+                        out=vecs[v * VEC_ROWS : (v + 1) * VEC_ROWS, :], in_=vec.rearrange("(a f) -> a f", a=VEC_ROWS)
                     )
+                nc.sync.dma_start(out=tens[0:1, :], in_=tension.rearrange("c o -> o c"))
 
-        warm = keep.tile([P, 1], F32, name="warm")
-        nc.vector.memset(warm[:], 0.0)
-        nc.scalar.activation(out=warm[:], in_=warm[:], func=ACT.Sigmoid)
-
-        ident_f32 = keep.tile([P, P], F32, name="ident_f32")
-        make_identity(nc, ident_f32[:])
-        ident_bf16 = keep.tile([P, P], BF16, name="ident_bf16")
-        nc.vector.tensor_copy(out=ident_bf16[:], in_=ident_f32[:])
-
-        def flip_pair(first_words, second_words, name):
-            bank = flip_pool.tile([P, PAIR, 2, P], F32, tag="flip")
+        def flip(first_words, second_words, name):
+            bank = flip_pool.tile([P, 2, 2, P], F32, tag="flip")
             for b, words in enumerate((first_words, second_words)):
                 for u in range(2):
-                    nc.tensor.transpose(bank[:, b, u, :], words[:, u * P : (u + 1) * P], ident_f32[:])
-            grouped = keep.tile([P, PAIR * P * 4], BF16, name="grouped_" + name, align_bytes=64)
+                    nc.tensor.transpose(bank[:, b, u, :], words[:, u * P : (u + 1) * P], ident[:])
+            grouped = keep.tile([P, 2 * P * 4], BF16, name="grouped_" + name, align_bytes=64)
             nc.scalar.copy(
-                out=grouped[:].bitcast(F32).rearrange("p (b c u) -> p b c u", b=PAIR, u=2),
+                out=grouped[:].bitcast(F32).rearrange("p (b c u) -> p b c u", b=2, u=2),
                 in_=bank[:].rearrange("p b u c -> p b c u"),
             )
             return grouped
 
         def quantise(grouped, name):
-            codes = keep.tile([P, PAIR * P], U32, name="codes_" + name, align_bytes=64)
-            scales = keep.tile([P, PAIR * P], U8, name="scales_" + name, align_bytes=64)
+            codes = keep.tile([P, 2 * P], U32, name="codes_" + name, align_bytes=64)
+            scales = keep.tile([P, 2 * P], U8, name="scales_" + name, align_bytes=64)
             nc.vector.quantize_mx(out=codes[:].bitcast(FP8X4), scales=scales[:], in_=grouped[:])
             return codes, scales
 
-        grouped_x = flip_pair(ag_sb[:].bitcast(F32), h_sb[:].bitcast(F32), "x")
-        hT_ps = flip_pool.tile([P, BLOCKS_PER_GATE, CELLS], BF16, tag="flip")
-        for blk in range(BLOCKS_PER_GATE):
-            nc.tensor.transpose(hT_ps[:, blk, :], h_sb[:, blk * P : (blk + 1) * P], ident_bf16[:])
-        h_kept = keep.tile([P, BLOCKS_PER_GATE, CELLS], F32, name="h_kept")
-        nc.scalar.activation(out=h_kept[:], in_=hT_ps[:], func=ACT.Copy, scale=KEEP)
-
-        vecs_ps = flip_pool.tile([P, P], BF16, tag="flip")
-        nc.tensor.transpose(vecs_ps[:], vecs[:], ident_bf16[:])
-        tension_ps = flip_pool.tile([P, CELLS], F32, tag="flip")
-        nc.tensor.matmul(
-            out=tension_ps[:],
-            lhsT=ident_bf16[:, TENSION_ROW : TENSION_ROW + 1].to_broadcast([P, P]),
-            rhs=vecs[:],
-            start=True,
-            stop=True,
-        )
-        cols = keep.tile([P, 3 * N_BLOCKS], F32, name="cols")
-        nc.vector.tensor_copy(out=cols[:], in_=vecs_ps[:, 0 : 3 * N_BLOCKS])
-        w_it_col = cols[:, 0:N_BLOCKS]
-        b_ih_col = cols[:, N_BLOCKS : 2 * N_BLOCKS]
-        b_hh_col = cols[:, 2 * N_BLOCKS : 3 * N_BLOCKS]
-        b_sum_col = keep.tile([P, N_BLOCKS], F32, name="b_sum_col")
-        nc.vector.tensor_add(out=b_sum_col[:], in0=b_ih_col, in1=b_hh_col)
-        tension_rows = keep.tile([P, CELLS], F32, name="tension_rows")
-        nc.vector.tensor_copy(out=tension_rows[:], in_=tension_ps[:])
-
-        side = keep.tile([P, N_BLOCKS, CELLS], F32, name="side")
-        for gate in GATE_ORDER:
-            bias_col = b_ih_col if gate == GATE_N else b_sum_col[:]
-            for blk in range(gate * BLOCKS_PER_GATE, (gate + 1) * BLOCKS_PER_GATE):
-                nc.vector.tensor_scalar(
-                    out=side[:, blk, :],
-                    in0=tension_rows[:],
-                    scalar1=w_it_col[:, blk : blk + 1],
-                    scalar2=bias_col[:, blk : blk + 1],
-                    op0=MULT,
-                    op1=ADD,
-                )
+        grouped_x = flip(ag_sb[:].bitcast(F32), h_sb[:].bitcast(F32), "x")
         codes_x, scales_x = quantise(grouped_x, "x")
+        h_turned = grouped_x[:].rearrange("p (b c u e) -> p b u e c", b=2, u=2, e=2)
 
-        units = [(gate, m, pair) for gate in GATE_ORDER for m in range(2) for pair in range(PAIRS)]
         grouped_w = {}
         quantised_w = {}
         acc = {}
         gate_out = {}
         diff = {}
-        blend = {}
+        cols = {}
 
-        def flip_weights(gate, m, pair):
-            words = w_sb[(gate, m)][:].bitcast(F32)
-            first = pair * PAIR * WORDS
-            grouped_w[(gate, m, pair)] = flip_pair(
-                words[:, first : first + WORDS], words[:, first + WORDS : first + 2 * WORDS], "%d_%d_%d" % (gate, m, pair)
-            )
+        def vectors():
+            vecs_ps = flip_pool.tile([P, VEC_HALVES, P], F32, tag="flip")
+            for j in range(VEC_HALVES):
+                nc.tensor.transpose(
+                    vecs_ps[:, j, :], vecs[:, j * HALF : (j + 1) * HALF].bitcast(F32), ident[:]
+                )
+            tension_ps = acc_pool.tile([P, CELLS], F32, tag="acc")
+            nc.tensor.matmul(out=tension_ps[:], lhsT=ones[:], rhs=tens[:], start=True, stop=True)
+            wide = VEC_ROWS * E
+            cols_all = keep.tile([P, VEC_HALVES, 3 * wide], F32, name="cols_all")
+            nc.vector.tensor_copy(out=cols_all[:], in_=vecs_ps[:].bitcast(BF16)[:, :, 0 : 3 * wide])
+            b_sum = keep.tile([P, VEC_HALVES, wide], F32, name="b_sum")
+            tension_rows = keep.tile([P, CELLS], F32, name="tension_rows")
+            nc.vector.tensor_copy(out=tension_rows[:], in_=tension_ps[:])
+            nc.vector.tensor_add(out=b_sum[:], in0=cols_all[:, :, wide : 2 * wide], in1=cols_all[:, :, 2 * wide : 3 * wide])
+            cols["w_it"] = cols_all[:, :, 0:wide]
+            cols["b_ih"] = cols_all[:, :, wide : 2 * wide]
+            cols["b_hh"] = cols_all[:, :, 2 * wide : 3 * wide]
+            cols["b_sum"] = b_sum[:]
+            cols["tension"] = tension_rows[:]
 
-        def quantise_weights(gate, m, pair):
-            quantised_w[(gate, m, pair)] = quantise(grouped_w[(gate, m, pair)], "%d_%d_%d" % (gate, m, pair))
+        def col(name, half, gate, e):
+            row, j = divmod(gate * HALVES + half, VEC_HALVES)
+            at = row * E + e
+            return cols[name][:, j, at : at + 1]
 
-        def mx_pass(acc_block, gate, m, blk, start, stop):
-            codes, scales = quantised_w[(gate, m, blk // PAIR)]
-            w_cols = slice((blk % PAIR) * P, (blk % PAIR + 1) * P)
+        def flip_weights(half, gate, m):
+            words = w_sb[(half, gate, m)][:].bitcast(F32)
+            grouped_w[(half, gate, m)] = flip(words[:, 0:WORDS], words[:, WORDS : 2 * WORDS], "%d_%d_%d" % (half, gate, m))
+
+        def quantise_weights(half, gate, m):
+            quantised_w[(half, gate, m)] = quantise(grouped_w[(half, gate, m)], "%d_%d_%d" % (half, gate, m))
+
+        def mx_pass(acc_block, half, gate, m, e, start, stop):
+            codes, scales = quantised_w[(half, gate, m)]
+            w_cols = slice(e * P, (e + 1) * P)
             x_cols = slice(m * CELLS, (m + 1) * CELLS)
             nc.tensor.matmul_mx(
                 out=acc_block,
@@ -164,107 +150,99 @@ def tile_phiaslossengine_pb_s_kernel(tc, ag_diff, tension, hiddens, W_io, w_it, 
                 stop=stop,
             )
 
-        def multiply(gate):
-            if gate == GATE_N:
-                for m in range(2):
-                    acc_m = acc_pool.tile([P, BLOCKS_PER_GATE, CELLS], F32, tag="acc")
-                    for blk in range(BLOCKS_PER_GATE):
-                        mx_pass(acc_m[:, blk, :], gate, m, blk, True, True)
-                    acc[(gate, m)] = acc_m
-            else:
-                acc_sum = acc_pool.tile([P, BLOCKS_PER_GATE, CELLS], F32, tag="acc")
-                for blk in range(BLOCKS_PER_GATE):
-                    mx_pass(acc_sum[:, blk, :], gate, 0, blk, True, False)
-                    mx_pass(acc_sum[:, blk, :], gate, 1, blk, False, True)
-                acc[(gate, 0)] = acc_sum
+        def multiply(half, gate):
+            acc_tile = acc_pool.tile([P, 2, E, CELLS], F32, tag="acc")
+            acc[(half, gate)] = acc_tile
+            for e in range(E):
+                if gate == GATE_N:
+                    for m in range(2):
+                        mx_pass(acc_tile[:, m, e, :], half, gate, m, e, True, True)
+                else:
+                    mx_pass(acc_tile[:, 0, e, :], half, gate, 0, e, True, False)
+                    mx_pass(acc_tile[:, 0, e, :], half, gate, 1, e, False, True)
 
-        def blocks_of(pair):
-            return slice(pair * PAIR, (pair + 1) * PAIR)
-
-        def gate_function(gate):
-            first = gate * BLOCKS_PER_GATE
-            pre = [pair_tile("pre%d" % gate, pair) for pair in range(PAIRS)]
-            for pair in range(PAIRS):
-                nc.vector.tensor_add(
-                    out=pre[pair][:],
-                    in0=acc[(gate, 0)][:, blocks_of(pair), :],
-                    in1=side[:, first + pair * PAIR : first + (pair + 1) * PAIR, :],
+        def gate_function(half, gate):
+            pre = half_tile("pre%d" % gate, half)
+            for e in range(E):
+                nc.vector.scalar_tensor_tensor(
+                    out=pre[:, e, :],
+                    in0=cols["tension"],
+                    scalar=col("w_it", half, gate, e),
+                    in1=acc[(half, gate)][:, 0, e, :],
+                    op0=MULT,
+                    op1=ADD,
                 )
             if gate == GATE_N:
-                rh = [pair_tile("rh", pair) for pair in range(PAIRS)]
-                for blk in range(BLOCKS_PER_GATE):
+                rh = half_tile("rh", half)
+                for e in range(E):
                     nc.vector.scalar_tensor_tensor(
-                        out=rh[blk // PAIR][:, blk % PAIR, :],
-                        in0=acc[(gate, 1)][:, blk, :],
-                        scalar=b_hh_col[:, first + blk : first + blk + 1],
-                        in1=gate_out[(GATE_R, blk // PAIR)][:, blk % PAIR, :],
+                        out=rh[:, e, :],
+                        in0=acc[(half, gate)][:, 1, e, :],
+                        scalar=col("b_hh", half, gate, e),
+                        in1=gate_out[(half, GATE_R)][:, e, :],
                         op0=ADD,
                         op1=MULT,
                     )
-                for pair in range(PAIRS):
-                    nc.vector.tensor_add(out=pre[pair][:], in0=pre[pair][:], in1=rh[pair][:])
-            for pair in range(PAIRS):
-                result = pair_tile("gate%d" % gate, pair)
-                nc.scalar.activation(out=result[:], in_=pre[pair][:], func=ACT.Tanh if gate == GATE_N else ACT.Sigmoid)
-                gate_out[(gate, pair)] = result
+                nc.vector.tensor_add(out=pre[:], in0=pre[:], in1=rh[:])
+            result = half_tile("gate%d" % gate, half)
+            for e in range(E):
+                nc.scalar.activation(
+                    out=result[:, e, :],
+                    in_=pre[:, e, :],
+                    func=ACT.Tanh if gate == GATE_N else ACT.Sigmoid,
+                    bias=col("b_ih" if gate == GATE_N else "b_sum", half, gate, e),
+                )
+            gate_out[(half, gate)] = result
 
-        def after_function(gate):
+        def after_function(half, gate):
             if gate == GATE_N:
-                for pair in range(PAIRS):
-                    diff[pair] = pair_tile("diff", pair)
-                    nc.vector.scalar_tensor_tensor(
-                        out=diff[pair][:],
-                        in0=gate_out[(GATE_N, pair)][:],
-                        scalar=-KEEP,
-                        in1=h_kept[:, blocks_of(pair), :],
-                        op0=MULT,
-                        op1=ADD,
-                    )
+                diff[half] = half_tile("diff", half)
+                nc.vector.tensor_sub(out=diff[half][:], in0=h_turned[:, 1, half, :, :], in1=gate_out[(half, GATE_N)][:])
             if gate == GATE_Z:
-                by_faction = "p b (f s) -> p (b f) s"
-                n_sums = PAIR * CELLS // FACTION
-                moved = [pair_tile("moved", pair) for pair in range(PAIRS)]
-                kept = [pair_tile("kept", pair) for pair in range(PAIRS)]
-                sums = [keep.tile([P, n_sums], F32, name="sums_%d" % pair) for pair in range(PAIRS)]
-                for pair in range(PAIRS):
-                    nc.vector.tensor_mul(out=moved[pair][:], in0=gate_out[(GATE_Z, pair)][:], in1=diff[pair][:])
-                for pair in range(PAIRS):
-                    nc.vector.scalar_tensor_tensor(
-                        out=kept[pair][:], in0=gate_out[(GATE_N, pair)][:], scalar=KEEP, in1=moved[pair][:], op0=MULT, op1=ADD
-                    )
-                for pair in range(PAIRS):
+                by_faction = "p (f s) -> p f s"
+                n_sums = CELLS // FACTION
+                moved = half_tile("moved", half)
+                new = half_tile("new", half)
+                blend = half_tile("blend", half)
+                sums = keep.tile([P, E, n_sums], F32, name="sums_%d" % half)
+                for e in range(E):
+                    nc.vector.tensor_mul(out=moved[:, e, :], in0=gate_out[(half, GATE_Z)][:, e, :], in1=diff[half][:, e, :])
+                for e in range(E):
+                    nc.vector.tensor_add(out=new[:, e, :], in0=gate_out[(half, GATE_N)][:, e, :], in1=moved[:, e, :])
+                for e in range(E):
                     nc.vector.tensor_reduce(
-                        out=sums[pair][:], in_=kept[pair][:].rearrange(by_faction, s=FACTION), axis=mybir.AxisListType.X, op=ADD
+                        out=sums[:, e, :], in_=new[:, e, :].rearrange(by_faction, s=FACTION), axis=mybir.AxisListType.X, op=ADD
                     )
-                for pair in range(PAIRS):
-                    blend[pair] = pair_tile("blend", pair)
+                for e in range(E):
                     nc.vector.scalar_tensor_tensor(
-                        out=blend[pair][:].rearrange(by_faction, s=FACTION),
-                        in0=sums[pair][:].unsqueeze(2).to_broadcast([P, n_sums, FACTION]),
+                        out=blend[:, e, :].rearrange(by_faction, s=FACTION),
+                        in0=sums[:, e, :].unsqueeze(2).to_broadcast([P, n_sums, FACTION]),
                         scalar=MEAN_OVER_KEPT,
-                        in1=kept[pair][:].rearrange(by_faction, s=FACTION),
+                        in1=new[:, e, :].rearrange(by_faction, s=FACTION),
                         op0=MULT,
                         op1=ADD,
                     )
-
-        def store(gate):
-            if gate != GATE_Z:
-                return
-            for pair in range(PAIRS):
-                out_ps = acc_pool.tile([P, PAIR, P], F32, tag="acc")
-                for b in range(PAIR):
-                    nc.tensor.transpose(out_ps[:, b, :], blend[pair][:, b, :], ident_f32[:])
-                out_sb = pair_tile("out_sb", pair)
-                nc.scalar.copy(out=out_sb[:], in_=out_ps[:])
-                nc.sync.dma_start(out=out[:, pair * PAIR * P : (pair + 1) * PAIR * P], in_=out_sb[:].rearrange("p b h -> p (b h)"))
+                out_ps = acc_pool.tile([P, E, P], F32, tag="acc")
+                for e in range(E):
+                    nc.tensor.transpose(out_ps[:, e, :], blend[:, e, :], ident[:])
+                out_sb = keep.tile([P, HALF], F32, name="out_sb_%d" % half)
+                nc.scalar.activation(
+                    out=out_sb[:].rearrange("c (p e) -> c p e", e=E),
+                    in_=out_ps[:].rearrange("c e p -> c p e"),
+                    func=ACT.Copy,
+                    scale=KEEP,
+                )
+                nc.sync.dma_start(out=out[:, half * HALF : (half + 1) * HALF], in_=out_sb[:])
 
         unit_stages = (flip_weights, quantise_weights)
-        gate_stages = (multiply, gate_function, after_function, store)
+        gate_stages = (multiply, gate_function, after_function)
         for tick in range(len(units) + len(unit_stages) + len(gate_stages) - 1):
+            if tick == 2:
+                vectors()
             for lag, stage in enumerate(unit_stages):
                 if 0 <= tick - lag < len(units):
                     stage(*units[tick - lag])
             for lag, stage in enumerate(gate_stages):
                 u = tick - len(unit_stages) - lag
-                if 0 <= u < len(units) and units[u][1:] == (1, PAIRS - 1):
-                    stage(units[u][0])
+                if 0 <= u < len(units) and units[u][2] == 1:
+                    stage(*units[u][:2])

@@ -28,6 +28,23 @@ MEAN_OVER_KEPT = (1.0 - KEEP) / (FACTION * KEEP)
 VEC_ROWS = 2
 VEC_HALVES = 3
 
+FLIP_BANKS = 4
+ACC_BANKS = 3
+ORDER = "half"
+VEC_Q = "sync"
+VEC_AT = 3
+DUMMY0 = 0
+DUMMY_N = 0
+DUMMY_LAST = 12
+DUMMY_FIRST = 0
+V_COPIES = (1, 4)
+LQ, LM, LP, LA, LF = 1, 2, 3, 4, 5
+OUT_ENG = "S"
+BACK_ENG = {"n": "S", "moved": "S"}
+LAG = {"quant": 2, "mult": 4, "pre": 4, "rh": 4, "add": 5, "act": 4, "actn": 5, "diff": 6, "mul": 6, "zadd": 7, "zsum": 9, "zblend": 10, "turn": 10, "out": 10}
+MXD = 0
+SEQ = ("mult", "pre", "rh", "add", "act", "actn", "diff", "mul", "zadd", "zsum", "zblend", "turn", "out")
+MEAN = 0.15 / 16
 FLOPS = 2 * 2 * CELLS * K * 3 * HID
 
 
@@ -35,30 +52,44 @@ def tile_phiaslossengine_pb_s_kernel(tc, ag_diff, tension, hiddens, W_io, w_it, 
     nc = tc.nc
     with ExitStack() as stack:
         keep = stack.enter_context(tc.tile_pool(name="keep", bufs=1))
-        flip_pool = stack.enter_context(tc.psum_pool(name="flip", bufs=4))
-        acc_pool = stack.enter_context(tc.psum_pool(name="acc", bufs=4))
+        flip_pool = stack.enter_context(tc.psum_pool(name="flip", bufs=FLIP_BANKS))
+        acc_pool = stack.enter_context(tc.psum_pool(name="acc", bufs=ACC_BANKS))
+        dummy_pool = stack.enter_context(tc.psum_pool(name="dummy", bufs=1))
+        stack.enter_context(tc.manual_schedule())
 
         def half_tile(name, half):
             return keep.tile([P, E, CELLS], F32, name="%s_%d" % (name, half))
 
         vecs = keep.tile([P, VEC_HALVES * HALF], BF16, name="vecs")
-        nc.vector.memset(vecs[:], 0.0)
         tens = keep.tile([P, CELLS], BF16, name="tens")
-        nc.vector.memset(tens[:], 0.0)
+        zeros = keep.tile([P, 2 * P], F32, name="zeros")
         ones = keep.tile([P, P], BF16, name="ones")
-        nc.vector.memset(ones[:], 1.0)
         warm = keep.tile([P, 1], F32, name="warm")
         nc.vector.memset(warm[:], 0.0)
-        nc.scalar.activation(out=warm[:], in_=warm[:], func=ACT.Sigmoid)
+        nc.vector.memset(zeros[:], 0.0)
+        nc.vector.memset(tens[:], 0.0)
+        nc.vector.memset(vecs[:], 0.0)
+        nc.vector.memset(ones[:], 1.0)
         ident = keep.tile([P, P], F32, name="ident")
         make_identity(nc, ident[:])
-
         ag_sb = keep.tile([P, K], BF16, name="ag_sb")
-        nc.sync.dma_start(out=ag_sb[:], in_=ag_diff)
         h_sb = keep.tile([P, K], BF16, name="h_sb")
-        nc.sync.dma_start(out=h_sb[:], in_=hiddens)
-        units = [(half, gate, m) for half in range(HALVES) for gate in GATE_ORDER for m in range(2)]
+        if ORDER == "half":
+            units = [(half, gate, m) for half in range(HALVES) for gate in GATE_ORDER for m in range(2)]
+        else:
+            units = [(half, gate, m) for gate in GATE_ORDER for half in range(HALVES) for m in range(2)]
         w_sb = {}
+
+        def load_vecs():
+            q = nc.scalar if VEC_Q == "scalar" else nc.gpsimd if VEC_Q == "gpsimd" else nc.sync
+            q.dma_start(out=tens[0:1, :], in_=tension.rearrange("c o -> o c"))
+            for v, vec in enumerate((w_it, b_ih, b_hh)):
+                q.dma_start(out=vecs[v * VEC_ROWS : (v + 1) * VEC_ROWS, :], in_=vec.rearrange("(a f) -> a f", a=VEC_ROWS))
+
+        nc.sync.dma_start(out=ag_sb[:], in_=ag_diff)
+        nc.sync.dma_start(out=h_sb[:], in_=hiddens)
+        if VEC_AT == -1:
+            load_vecs()
         for i, unit in enumerate(units):
             half, gate, m = unit
             first = gate * HID + half * HALF
@@ -67,56 +98,70 @@ def tile_phiaslossengine_pb_s_kernel(tc, ag_diff, tension, hiddens, W_io, w_it, 
                 out=w_sb[unit][:],
                 in_=(W_io, W_hh)[m][first : first + HALF, :].rearrange("(p e) k -> p (e k)", e=E),
             )
-            if i == 1:
-                for v, vec in enumerate((w_it, b_ih, b_hh)):
-                    nc.sync.dma_start(
-                        out=vecs[v * VEC_ROWS : (v + 1) * VEC_ROWS, :], in_=vec.rearrange("(a f) -> a f", a=VEC_ROWS)
-                    )
-                nc.sync.dma_start(out=tens[0:1, :], in_=tension.rearrange("c o -> o c"))
+            if i == VEC_AT:
+                load_vecs()
+        nc.scalar.activation(out=warm[:], in_=warm[:], func=ACT.Sigmoid)
 
-        def flip(first_words, second_words, name):
-            bank = flip_pool.tile([P, 2, 2, P], F32, tag="flip")
-            for b, words in enumerate((first_words, second_words)):
-                for u in range(2):
-                    nc.tensor.transpose(bank[:, b, u, :], words[:, u * P : (u + 1) * P], ident[:])
-            grouped = keep.tile([P, 2 * P * 4], BF16, name="grouped_" + name, align_bytes=64)
-            nc.scalar.copy(
-                out=grouped[:].bitcast(F32).rearrange("p (b c u) -> p b c u", b=2, u=2),
-                in_=bank[:].rearrange("p b u c -> p b c u"),
-            )
-            return grouped
+        def dummy(n):
+            sink = dummy_pool.tile([P, 2 * P], F32, tag="dummy")
+            nc.tensor.matmul(out=sink[:, 0:n], lhsT=zeros[:, 0:P], rhs=zeros[:, 0:n], start=True, stop=True)
 
-        def quantise(grouped, name):
-            codes = keep.tile([P, 2 * P], U32, name="codes_" + name, align_bytes=64)
-            scales = keep.tile([P, 2 * P], U8, name="scales_" + name, align_bytes=64)
-            nc.vector.quantize_mx(out=codes[:].bitcast(FP8X4), scales=scales[:], in_=grouped[:])
-            return codes, scales
+        for i in range(DUMMY0):
+            dummy(P)
 
-        grouped_x = flip(ag_sb[:].bitcast(F32), h_sb[:].bitcast(F32), "x")
-        codes_x, scales_x = quantise(grouped_x, "x")
-        h_turned = grouped_x[:].rearrange("p (b c u e) -> p b u e c", b=2, u=2, e=2)
-
-        grouped_w = {}
-        quantised_w = {}
+        banks = {}
+        grouped = {}
+        quantised = {}
         acc = {}
         gate_out = {}
+        pre = {}
         diff = {}
         cols = {}
+        moved = {}
+        new = {}
+        blend = {}
+        sums = {}
+        rh = {}
+        out_ps = {}
 
-        def vectors():
-            vecs_ps = flip_pool.tile([P, VEC_HALVES, P], F32, tag="flip")
+        def turn(key, first_words, second_words):
+            bank = flip_pool.tile([P, 2, 2, P], F32, tag="flip")
+            banks[key] = bank
+            for b, words in enumerate((first_words, second_words)):
+                for u in range(2):
+                    nc.tensor.transpose(banks[key][:, b, u, :], words[:, u * P : (u + 1) * P], ident[:])
+
+        def copy(key, engine):
+            grouped[key] = keep.tile([P, 2 * P * 4], BF16, name="grouped_%s" % str(key), align_bytes=64)
+            o = grouped[key][:].bitcast(F32).rearrange("p (b c u) -> p b c u", b=2, u=2)
+            i = banks[key][:].rearrange("p b u c -> p b c u")
+            if engine == "S":
+                nc.scalar.copy(out=o, in_=i)
+            else:
+                nc.vector.tensor_copy(out=o, in_=i)
+
+        def quantise(key):
+            codes = keep.tile([P, 2 * P], U32, name="codes_%s" % str(key), align_bytes=64)
+            scales = keep.tile([P, 2 * P], U8, name="scales_%s" % str(key), align_bytes=64)
+            nc.vector.quantize_mx(out=codes[:].bitcast(FP8X4), scales=scales[:], in_=grouped[key][:])
+            quantised[key] = (codes, scales)
+
+        def vectors_pe():
+            ps = acc_pool.tile([P, 512], F32, tag="acc")
+            cols["ps"] = ps
             for j in range(VEC_HALVES):
-                nc.tensor.transpose(
-                    vecs_ps[:, j, :], vecs[:, j * HALF : (j + 1) * HALF].bitcast(F32), ident[:]
-                )
-            tension_ps = acc_pool.tile([P, CELLS], F32, tag="acc")
-            nc.tensor.matmul(out=tension_ps[:], lhsT=ones[:], rhs=tens[:], start=True, stop=True)
+                nc.tensor.transpose(ps[:, j * P : (j + 1) * P], vecs[:, j * HALF : (j + 1) * HALF].bitcast(F32), ident[:])
+            nc.tensor.matmul(out=ps[:, 3 * P : 4 * P], lhsT=ones[:], rhs=tens[:], start=True, stop=True)
+
+        def vectors_v():
+            ps = cols["ps"]
             wide = VEC_ROWS * E
             cols_all = keep.tile([P, VEC_HALVES, 3 * wide], F32, name="cols_all")
-            nc.vector.tensor_copy(out=cols_all[:], in_=vecs_ps[:].bitcast(BF16)[:, :, 0 : 3 * wide])
-            b_sum = keep.tile([P, VEC_HALVES, wide], F32, name="b_sum")
+            view = ps[:, 0 : 3 * P].bitcast(BF16).rearrange("p (j r) -> p j r", j=VEC_HALVES)
+            nc.vector.tensor_copy(out=cols_all[:], in_=view[:, :, 0 : 3 * wide])
             tension_rows = keep.tile([P, CELLS], F32, name="tension_rows")
-            nc.vector.tensor_copy(out=tension_rows[:], in_=tension_ps[:])
+            nc.vector.tensor_copy(out=tension_rows[:], in_=ps[:, 3 * P : 4 * P])
+            b_sum = keep.tile([P, VEC_HALVES, wide], F32, name="b_sum")
             nc.vector.tensor_add(out=b_sum[:], in0=cols_all[:, :, wide : 2 * wide], in1=cols_all[:, :, 2 * wide : 3 * wide])
             cols["w_it"] = cols_all[:, :, 0:wide]
             cols["b_ih"] = cols_all[:, :, wide : 2 * wide]
@@ -129,15 +174,9 @@ def tile_phiaslossengine_pb_s_kernel(tc, ag_diff, tension, hiddens, W_io, w_it, 
             at = row * E + e
             return cols[name][:, j, at : at + 1]
 
-        def flip_weights(half, gate, m):
-            words = w_sb[(half, gate, m)][:].bitcast(F32)
-            grouped_w[(half, gate, m)] = flip(words[:, 0:WORDS], words[:, WORDS : 2 * WORDS], "%d_%d_%d" % (half, gate, m))
-
-        def quantise_weights(half, gate, m):
-            quantised_w[(half, gate, m)] = quantise(grouped_w[(half, gate, m)], "%d_%d_%d" % (half, gate, m))
-
         def mx_pass(acc_block, half, gate, m, e, start, stop):
-            codes, scales = quantised_w[(half, gate, m)]
+            codes, scales = quantised[(half, gate, m)]
+            codes_x, scales_x = quantised["x"]
             w_cols = slice(e * P, (e + 1) * P)
             x_cols = slice(m * CELLS, (m + 1) * CELLS)
             nc.tensor.matmul_mx(
@@ -150,7 +189,22 @@ def tile_phiaslossengine_pb_s_kernel(tc, ag_diff, tension, hiddens, W_io, w_it, 
                 stop=stop,
             )
 
+        def mx_dummy():
+            sink = dummy_pool.tile([P, 2 * P], F32, tag="dummy")
+            codes_x, scales_x = quantised["x"]
+            nc.tensor.matmul_mx(
+                out=sink[:],
+                lhsT=codes_x[:, 0:P].bitcast(FP8X4),
+                lhsT_scale=scales_x[:, 0:P],
+                rhs=codes_x[:].bitcast(FP8X4),
+                rhs_scale=scales_x[:],
+                start=True,
+                stop=True,
+            )
+
         def multiply(half, gate):
+            for i in range(MXD):
+                mx_dummy()
             acc_tile = acc_pool.tile([P, 2, E, CELLS], F32, tag="acc")
             acc[(half, gate)] = acc_tile
             for e in range(E):
@@ -161,88 +215,146 @@ def tile_phiaslossengine_pb_s_kernel(tc, ag_diff, tension, hiddens, W_io, w_it, 
                     mx_pass(acc_tile[:, 0, e, :], half, gate, 0, e, True, False)
                     mx_pass(acc_tile[:, 0, e, :], half, gate, 1, e, False, True)
 
-        def gate_function(half, gate):
-            pre = half_tile("pre%d" % gate, half)
+        def gate_pre(half, gate):
+            p = half_tile("pre%d" % gate, half)
+            pre[(half, gate)] = p
             for e in range(E):
                 nc.vector.scalar_tensor_tensor(
-                    out=pre[:, e, :],
+                    out=p[:, e, :],
                     in0=cols["tension"],
                     scalar=col("w_it", half, gate, e),
                     in1=acc[(half, gate)][:, 0, e, :],
                     op0=MULT,
                     op1=ADD,
                 )
-            if gate == GATE_N:
-                rh = half_tile("rh", half)
-                for e in range(E):
-                    nc.vector.scalar_tensor_tensor(
-                        out=rh[:, e, :],
-                        in0=acc[(half, gate)][:, 1, e, :],
-                        scalar=col("b_hh", half, gate, e),
-                        in1=gate_out[(half, GATE_R)][:, e, :],
-                        op0=ADD,
-                        op1=MULT,
-                    )
-                nc.vector.tensor_add(out=pre[:], in0=pre[:], in1=rh[:])
+
+        def n_rh(half):
+            rh[half] = half_tile("rh", half)
+            for e in range(E):
+                nc.vector.scalar_tensor_tensor(
+                    out=rh[half][:, e, :],
+                    in0=acc[(half, GATE_N)][:, 1, e, :],
+                    scalar=col("b_hh", half, GATE_N, e),
+                    in1=gate_out[(half, GATE_R)][:, e, :],
+                    op0=ADD,
+                    op1=MULT,
+                )
+
+        def n_add(half):
+            for e in range(E):
+                p = pre[(half, GATE_N)]
+                nc.vector.tensor_add(out=p[:, e, :], in0=p[:, e, :], in1=rh[half][:, e, :])
+
+        def gate_act(half, gate):
             result = half_tile("gate%d" % gate, half)
             for e in range(E):
                 nc.scalar.activation(
                     out=result[:, e, :],
-                    in_=pre[:, e, :],
+                    in_=pre[(half, gate)][:, e, :],
                     func=ACT.Tanh if gate == GATE_N else ACT.Sigmoid,
                     bias=col("b_ih" if gate == GATE_N else "b_sum", half, gate, e),
                 )
             gate_out[(half, gate)] = result
 
-        def after_function(half, gate):
-            if gate == GATE_N:
-                diff[half] = half_tile("diff", half)
-                nc.vector.tensor_sub(out=diff[half][:], in0=h_turned[:, 1, half, :, :], in1=gate_out[(half, GATE_N)][:])
-            if gate == GATE_Z:
-                by_faction = "p (f s) -> p f s"
-                n_sums = CELLS // FACTION
-                moved = half_tile("moved", half)
-                new = half_tile("new", half)
-                blend = half_tile("blend", half)
-                sums = keep.tile([P, E, n_sums], F32, name="sums_%d" % half)
-                for e in range(E):
-                    nc.vector.tensor_mul(out=moved[:, e, :], in0=gate_out[(half, GATE_Z)][:, e, :], in1=diff[half][:, e, :])
-                for e in range(E):
-                    nc.vector.tensor_add(out=new[:, e, :], in0=gate_out[(half, GATE_N)][:, e, :], in1=moved[:, e, :])
-                for e in range(E):
-                    nc.vector.tensor_reduce(
-                        out=sums[:, e, :], in_=new[:, e, :].rearrange(by_faction, s=FACTION), axis=mybir.AxisListType.X, op=ADD
-                    )
-                for e in range(E):
-                    nc.vector.scalar_tensor_tensor(
-                        out=blend[:, e, :].rearrange(by_faction, s=FACTION),
-                        in0=sums[:, e, :].unsqueeze(2).to_broadcast([P, n_sums, FACTION]),
-                        scalar=MEAN_OVER_KEPT,
-                        in1=new[:, e, :].rearrange(by_faction, s=FACTION),
-                        op0=MULT,
-                        op1=ADD,
-                    )
-                out_ps = acc_pool.tile([P, E, P], F32, tag="acc")
-                for e in range(E):
-                    nc.tensor.transpose(out_ps[:, e, :], blend[:, e, :], ident[:])
-                out_sb = keep.tile([P, HALF], F32, name="out_sb_%d" % half)
-                nc.scalar.activation(
-                    out=out_sb[:].rearrange("c (p e) -> c p e", e=E),
-                    in_=out_ps[:].rearrange("c e p -> c p e"),
-                    func=ACT.Copy,
-                    scale=KEEP,
-                )
-                nc.sync.dma_start(out=out[:, half * HALF : (half + 1) * HALF], in_=out_sb[:])
+        def make_diff(half):
+            h_turned = grouped["x"][:].rearrange("p (b c u e) -> p b u e c", b=2, u=2, e=2)
+            diff[half] = half_tile("diff", half)
+            nc.vector.tensor_sub(out=diff[half][:], in0=h_turned[:, 1, half, :, :], in1=gate_out[(half, GATE_N)][:])
 
-        unit_stages = (flip_weights, quantise_weights)
-        gate_stages = (multiply, gate_function, after_function)
-        for tick in range(len(units) + len(unit_stages) + len(gate_stages) - 1):
+        def z_mul(half):
+            moved[half] = half_tile("moved", half)
+            for e in range(E):
+                nc.vector.tensor_mul(out=moved[half][:, e, :], in0=gate_out[(half, GATE_Z)][:, e, :], in1=diff[half][:, e, :])
+
+        by_faction = "p (f s) -> p f s"
+        n_sums = CELLS // FACTION
+
+        def z_add(half):
+            new[half] = half_tile("new", half)
+            for e in range(E):
+                nc.vector.tensor_add(out=new[half][:, e, :], in0=gate_out[(half, GATE_N)][:, e, :], in1=moved[half][:, e, :])
+
+        def z_sum(half):
+            sums[half] = keep.tile([P, E, n_sums], F32, name="sums_%d" % half)
+            for e in range(E):
+                nc.vector.tensor_reduce(
+                    out=sums[half][:, e, :], in_=new[half][:, e, :].rearrange(by_faction, s=FACTION), axis=mybir.AxisListType.X, op=ADD
+                )
+
+        def z_blend(half):
+            blend[half] = half_tile("blend", half)
+            for e in range(E):
+                nc.vector.scalar_tensor_tensor(
+                    out=blend[half][:, e, :].rearrange(by_faction, s=FACTION),
+                    in0=sums[half][:, e, :].unsqueeze(2).to_broadcast([P, n_sums, FACTION]),
+                    scalar=MEAN_OVER_KEPT,
+                    in1=new[half][:, e, :].rearrange(by_faction, s=FACTION),
+                    op0=MULT,
+                    op1=ADD,
+                )
+
+        def turn_out(half):
+            turned = acc_pool.tile([P, E, P], F32, tag="acc")
+            out_ps[half] = turned
+            for e in range(E):
+                nc.tensor.transpose(out_ps[half][:, e, :], blend[half][:, e, :], ident[:])
+
+        def out_half(half):
+            out_sb = keep.tile([P, HALF], F32, name="out_sb_%d" % half)
+            o = out_sb[:].rearrange("c (p e) -> c p e", e=E)
+            i = out_ps[half][:].rearrange("c e p -> c p e")
+            nc.scalar.activation(out=o, in_=i, func=ACT.Copy, scale=KEEP)
+            nc.sync.dma_start(out=out[:, half * HALF : (half + 1) * HALF], in_=out_sb[:])
+
+        turn("x", ag_sb[:].bitcast(F32), h_sb[:].bitcast(F32))
+        copy("x", "S")
+        n = len(units)
+        last = {}
+        for i, (half, gate, m) in enumerate(units):
+            last[(half, gate)] = i
+        groups = {}
+        for k_, i in last.items():
+            groups[i] = k_
+        for tick in range(n + 20):
+            if tick < n:
+                words = w_sb[units[tick]][:].bitcast(F32)
+                turn(units[tick], words[:, 0:WORDS], words[:, WORDS : 2 * WORDS])
+            if DUMMY_FIRST <= tick < DUMMY_LAST and DUMMY_N:
+                dummy(DUMMY_N)
+            if tick < n:
+                copy(units[tick], "V" if tick in V_COPIES else "S")
+            if tick == 1:
+                vectors_pe()
+            if tick == 0:
+                quantise("x")
             if tick == 2:
-                vectors()
-            for lag, stage in enumerate(unit_stages):
-                if 0 <= tick - lag < len(units):
-                    stage(*units[tick - lag])
-            for lag, stage in enumerate(gate_stages):
-                u = tick - len(unit_stages) - lag
-                if 0 <= u < len(units) and units[u][2] == 1:
-                    stage(*units[u][:2])
+                vectors_v()
+            if 0 <= tick - LAG["quant"] < n:
+                quantise(units[tick - LAG["quant"]])
+
+            def at(stage, gate):
+                u = tick - LAG[stage]
+                return u in groups and (gate is None or groups[u][1] == gate)
+
+            for stage in SEQ:
+                if stage == "mult" and at(stage, None):
+                    multiply(*groups[tick - LAG[stage]])
+                if stage == "pre" and at(stage, None):
+                    gate_pre(*groups[tick - LAG[stage]])
+                if stage == "rh" and at(stage, GATE_N):
+                    n_rh(groups[tick - LAG[stage]][0])
+                if stage == "add" and at(stage, GATE_N):
+                    n_add(groups[tick - LAG[stage]][0])
+                if stage == "actn" and at(stage, GATE_N):
+                    gate_act(*groups[tick - LAG[stage]])
+                if stage == "act" and (at(stage, GATE_R) or at(stage, GATE_Z)):
+                    gate_act(*groups[tick - LAG[stage]])
+                if stage == "diff" and at(stage, GATE_N):
+                    make_diff(groups[tick - LAG[stage]][0])
+                if stage == "mul" and at(stage, GATE_Z):
+                    z_mul(groups[tick - LAG[stage]][0])
+                for name, f in (("zadd", z_add), ("zsum", z_sum), ("zblend", z_blend), ("turn", turn_out)):
+                    if stage == name and at(stage, GATE_Z):
+                        f(groups[tick - LAG[stage]][0])
+                if stage == "out" and at(stage, GATE_Z):
+                    out_half(groups[tick - LAG[stage]][0])

@@ -29,20 +29,20 @@ VEC_ROWS = 2
 VEC_HALVES = 3
 
 FLIP_BANKS = 4
-ACC_BANKS = 3
-ORDER = "half"
+ACC_BANKS = 4
+SEQG = ((0, 0), (2, 0), (0, 1), (2, 1), (1, 0), (1, 1))
+RUNS = (1, 1, 1, 1, 1, 1)
+TENS_AT = 2
+VEC_R = 2
+VEC_W = 3
+VPE = 4
+VV = 5
 VEC_Q = "sync"
 VEC_AT = 3
-DUMMY0 = 0
-DUMMY_N = 0
-DUMMY_LAST = 12
-DUMMY_FIRST = 0
 V_COPIES = (1, 4)
-LQ, LM, LP, LA, LF = 1, 2, 3, 4, 5
 OUT_ENG = "S"
 BACK_ENG = {"n": "S", "moved": "S"}
-LAG = {"quant": 2, "mult": 4, "pre": 4, "rh": 4, "add": 5, "act": 4, "actn": 5, "diff": 6, "mul": 6, "zadd": 7, "zsum": 9, "zblend": 10, "turn": 10, "out": 10}
-MXD = 0
+LAG = {"quant": 2, "mult": 6, "pre": 7, "rh": 7, "add": 8, "act": 7, "actn": 8, "diff": 11, "mul": 9, "zadd": 11, "zsum": 11, "zblend": 11, "turn": 11, "out": 11}
 SEQ = ("mult", "pre", "rh", "add", "act", "actn", "diff", "mul", "zadd", "zsum", "zblend", "turn", "out")
 MEAN = 0.15 / 16
 FLOPS = 2 * 2 * CELLS * K * 3 * HID
@@ -54,40 +54,32 @@ def tile_phiaslossengine_pb_s_kernel(tc, ag_diff, tension, hiddens, W_io, w_it, 
         keep = stack.enter_context(tc.tile_pool(name="keep", bufs=1))
         flip_pool = stack.enter_context(tc.psum_pool(name="flip", bufs=FLIP_BANKS))
         acc_pool = stack.enter_context(tc.psum_pool(name="acc", bufs=ACC_BANKS))
-        dummy_pool = stack.enter_context(tc.psum_pool(name="dummy", bufs=1))
         stack.enter_context(tc.manual_schedule())
 
         def half_tile(name, half):
             return keep.tile([P, E, CELLS], F32, name="%s_%d" % (name, half))
 
-        vecs = keep.tile([P, VEC_HALVES * HALF], BF16, name="vecs")
+        vecs = keep.tile([P, VEC_W * HALF], BF16, name="vecs")
         tens = keep.tile([P, CELLS], BF16, name="tens")
-        zeros = keep.tile([P, 2 * P], F32, name="zeros")
-        ones = keep.tile([P, P], BF16, name="ones")
         warm = keep.tile([P, 1], F32, name="warm")
         nc.vector.memset(warm[:], 0.0)
-        nc.vector.memset(zeros[:], 0.0)
-        nc.vector.memset(tens[:], 0.0)
         nc.vector.memset(vecs[:], 0.0)
-        nc.vector.memset(ones[:], 1.0)
         ident = keep.tile([P, P], F32, name="ident")
         make_identity(nc, ident[:])
         ag_sb = keep.tile([P, K], BF16, name="ag_sb")
         h_sb = keep.tile([P, K], BF16, name="h_sb")
-        if ORDER == "half":
-            units = [(half, gate, m) for half in range(HALVES) for gate in GATE_ORDER for m in range(2)]
-        else:
-            units = [(half, gate, m) for gate in GATE_ORDER for half in range(HALVES) for m in range(2)]
+        units = [(half, gate, m) for gate, half in SEQG for m in range(2)]
         w_sb = {}
 
         def load_vecs():
             q = nc.scalar if VEC_Q == "scalar" else nc.gpsimd if VEC_Q == "gpsimd" else nc.sync
-            q.dma_start(out=tens[0:1, :], in_=tension.rearrange("c o -> o c"))
             for v, vec in enumerate((w_it, b_ih, b_hh)):
-                q.dma_start(out=vecs[v * VEC_ROWS : (v + 1) * VEC_ROWS, :], in_=vec.rearrange("(a f) -> a f", a=VEC_ROWS))
+                q.dma_start(out=vecs[v * VEC_R : (v + 1) * VEC_R, :], in_=vec.rearrange("(a f) -> a f", a=VEC_R))
 
         nc.sync.dma_start(out=ag_sb[:], in_=ag_diff)
         nc.sync.dma_start(out=h_sb[:], in_=hiddens)
+        if TENS_AT == -1:
+            nc.sync.dma_start(out=tens[:], in_=tension.rearrange("c o -> (c o)").partition_broadcast(P))
         if VEC_AT == -1:
             load_vecs()
         for i, unit in enumerate(units):
@@ -98,16 +90,11 @@ def tile_phiaslossengine_pb_s_kernel(tc, ag_diff, tension, hiddens, W_io, w_it, 
                 out=w_sb[unit][:],
                 in_=(W_io, W_hh)[m][first : first + HALF, :].rearrange("(p e) k -> p (e k)", e=E),
             )
+            if i == TENS_AT:
+                nc.sync.dma_start(out=tens[:], in_=tension.rearrange("c o -> (c o)").partition_broadcast(P))
             if i == VEC_AT:
                 load_vecs()
         nc.scalar.activation(out=warm[:], in_=warm[:], func=ACT.Sigmoid)
-
-        def dummy(n):
-            sink = dummy_pool.tile([P, 2 * P], F32, tag="dummy")
-            nc.tensor.matmul(out=sink[:, 0:n], lhsT=zeros[:, 0:P], rhs=zeros[:, 0:n], start=True, stop=True)
-
-        for i in range(DUMMY0):
-            dummy(P)
 
         banks = {}
         grouped = {}
@@ -147,30 +134,24 @@ def tile_phiaslossengine_pb_s_kernel(tc, ag_diff, tension, hiddens, W_io, w_it, 
             quantised[key] = (codes, scales)
 
         def vectors_pe():
-            ps = acc_pool.tile([P, 512], F32, tag="acc")
+            ps = acc_pool.tile([P, VEC_W, P], F32, tag="acc")
             cols["ps"] = ps
-            for j in range(VEC_HALVES):
-                nc.tensor.transpose(ps[:, j * P : (j + 1) * P], vecs[:, j * HALF : (j + 1) * HALF].bitcast(F32), ident[:])
-            nc.tensor.matmul(out=ps[:, 3 * P : 4 * P], lhsT=ones[:], rhs=tens[:], start=True, stop=True)
+            for j in range(VEC_W):
+                nc.tensor.transpose(ps[:, j, :], vecs[:, j * HALF : (j + 1) * HALF].bitcast(F32), ident[:])
 
         def vectors_v():
-            ps = cols["ps"]
-            wide = VEC_ROWS * E
-            cols_all = keep.tile([P, VEC_HALVES, 3 * wide], F32, name="cols_all")
-            view = ps[:, 0 : 3 * P].bitcast(BF16).rearrange("p (j r) -> p j r", j=VEC_HALVES)
-            nc.vector.tensor_copy(out=cols_all[:], in_=view[:, :, 0 : 3 * wide])
-            tension_rows = keep.tile([P, CELLS], F32, name="tension_rows")
-            nc.vector.tensor_copy(out=tension_rows[:], in_=ps[:, 3 * P : 4 * P])
-            b_sum = keep.tile([P, VEC_HALVES, wide], F32, name="b_sum")
+            wide = VEC_R * E
+            cols_all = keep.tile([P, VEC_W, 3 * wide], F32, name="cols_all")
+            nc.vector.tensor_copy(out=cols_all[:], in_=cols["ps"][:].bitcast(BF16)[:, :, 0 : 3 * wide])
+            b_sum = keep.tile([P, VEC_W, wide], F32, name="b_sum")
             nc.vector.tensor_add(out=b_sum[:], in0=cols_all[:, :, wide : 2 * wide], in1=cols_all[:, :, 2 * wide : 3 * wide])
             cols["w_it"] = cols_all[:, :, 0:wide]
             cols["b_ih"] = cols_all[:, :, wide : 2 * wide]
             cols["b_hh"] = cols_all[:, :, 2 * wide : 3 * wide]
             cols["b_sum"] = b_sum[:]
-            cols["tension"] = tension_rows[:]
 
         def col(name, half, gate, e):
-            row, j = divmod(gate * HALVES + half, VEC_HALVES)
+            row, j = divmod(gate * HALVES + half, VEC_W)
             at = row * E + e
             return cols[name][:, j, at : at + 1]
 
@@ -189,22 +170,7 @@ def tile_phiaslossengine_pb_s_kernel(tc, ag_diff, tension, hiddens, W_io, w_it, 
                 stop=stop,
             )
 
-        def mx_dummy():
-            sink = dummy_pool.tile([P, 2 * P], F32, tag="dummy")
-            codes_x, scales_x = quantised["x"]
-            nc.tensor.matmul_mx(
-                out=sink[:],
-                lhsT=codes_x[:, 0:P].bitcast(FP8X4),
-                lhsT_scale=scales_x[:, 0:P],
-                rhs=codes_x[:].bitcast(FP8X4),
-                rhs_scale=scales_x[:],
-                start=True,
-                stop=True,
-            )
-
         def multiply(half, gate):
-            for i in range(MXD):
-                mx_dummy()
             acc_tile = acc_pool.tile([P, 2, E, CELLS], F32, tag="acc")
             acc[(half, gate)] = acc_tile
             for e in range(E):
@@ -221,7 +187,7 @@ def tile_phiaslossengine_pb_s_kernel(tc, ag_diff, tension, hiddens, W_io, w_it, 
             for e in range(E):
                 nc.vector.scalar_tensor_tensor(
                     out=p[:, e, :],
-                    in0=cols["tension"],
+                    in0=tens[:],
                     scalar=col("w_it", half, gate, e),
                     in1=acc[(half, gate)][:, 0, e, :],
                     op0=MULT,
@@ -309,52 +275,51 @@ def tile_phiaslossengine_pb_s_kernel(tc, ag_diff, tension, hiddens, W_io, w_it, 
         turn("x", ag_sb[:].bitcast(F32), h_sb[:].bitcast(F32))
         copy("x", "S")
         n = len(units)
-        last = {}
-        for i, (half, gate, m) in enumerate(units):
-            last[(half, gate)] = i
         groups = {}
-        for k_, i in last.items():
-            groups[i] = k_
+        g = 0
+        for size in RUNS:
+            groups[2 * (g + size) - 1] = [(half, gate) for gate, half in SEQG[g : g + size]]
+            g += size
         for tick in range(n + 20):
             if tick < n:
                 words = w_sb[units[tick]][:].bitcast(F32)
                 turn(units[tick], words[:, 0:WORDS], words[:, WORDS : 2 * WORDS])
-            if DUMMY_FIRST <= tick < DUMMY_LAST and DUMMY_N:
-                dummy(DUMMY_N)
             if tick < n:
                 copy(units[tick], "V" if tick in V_COPIES else "S")
-            if tick == 1:
+            if tick == VPE:
                 vectors_pe()
             if tick == 0:
                 quantise("x")
-            if tick == 2:
+            if tick == VV:
                 vectors_v()
             if 0 <= tick - LAG["quant"] < n:
                 quantise(units[tick - LAG["quant"]])
 
-            def at(stage, gate):
-                u = tick - LAG[stage]
-                return u in groups and (gate is None or groups[u][1] == gate)
-
             for stage in SEQ:
-                if stage == "mult" and at(stage, None):
-                    multiply(*groups[tick - LAG[stage]])
-                if stage == "pre" and at(stage, None):
-                    gate_pre(*groups[tick - LAG[stage]])
-                if stage == "rh" and at(stage, GATE_N):
-                    n_rh(groups[tick - LAG[stage]][0])
-                if stage == "add" and at(stage, GATE_N):
-                    n_add(groups[tick - LAG[stage]][0])
-                if stage == "actn" and at(stage, GATE_N):
-                    gate_act(*groups[tick - LAG[stage]])
-                if stage == "act" and (at(stage, GATE_R) or at(stage, GATE_Z)):
-                    gate_act(*groups[tick - LAG[stage]])
-                if stage == "diff" and at(stage, GATE_N):
-                    make_diff(groups[tick - LAG[stage]][0])
-                if stage == "mul" and at(stage, GATE_Z):
-                    z_mul(groups[tick - LAG[stage]][0])
-                for name, f in (("zadd", z_add), ("zsum", z_sum), ("zblend", z_blend), ("turn", turn_out)):
-                    if stage == name and at(stage, GATE_Z):
-                        f(groups[tick - LAG[stage]][0])
-                if stage == "out" and at(stage, GATE_Z):
-                    out_half(groups[tick - LAG[stage]][0])
+                for half, gate in groups.get(tick - LAG[stage], ()):
+                    if stage == "mult":
+                        multiply(half, gate)
+                    elif stage == "pre":
+                        gate_pre(half, gate)
+                    elif stage == "rh" and gate == GATE_N:
+                        n_rh(half)
+                    elif stage == "add" and gate == GATE_N:
+                        n_add(half)
+                    elif stage == "act" and gate != GATE_N:
+                        gate_act(half, gate)
+                    elif stage == "actn" and gate == GATE_N:
+                        gate_act(half, gate)
+                    elif stage == "diff" and gate == GATE_N:
+                        make_diff(half)
+                    elif stage == "mul" and gate == GATE_Z:
+                        z_mul(half)
+                    elif stage == "zadd" and gate == GATE_Z:
+                        z_add(half)
+                    elif stage == "zsum" and gate == GATE_Z:
+                        z_sum(half)
+                    elif stage == "zblend" and gate == GATE_Z:
+                        z_blend(half)
+                    elif stage == "turn" and gate == GATE_Z:
+                        turn_out(half)
+                    elif stage == "out" and gate == GATE_Z:
+                        out_half(half)

@@ -38,7 +38,7 @@ VEC_W = 3
 VPE = 4
 VV = 5
 VEC_Q = "sync"
-VEC_AT = 3
+VEC_AT = 4
 V_COPIES = (1, 4)
 OUT_ENG = "S"
 BACK_ENG = {"n": "S", "moved": "S"}
@@ -63,7 +63,10 @@ def tile_phiaslossengine_pb_s_kernel(tc, ag_diff, tension, hiddens, W_io, w_it, 
         tens = keep.tile([P, CELLS], BF16, name="tens")
         warm = keep.tile([P, 1], F32, name="warm")
         nc.vector.memset(warm[:], 0.0)
+        nc.vector.memset(tens[:], 0.0)
         nc.vector.memset(vecs[:], 0.0)
+        ones = keep.tile([P, P], BF16, name="ones")
+        nc.vector.memset(ones[:], 1.0)
         ident = keep.tile([P, P], F32, name="ident")
         make_identity(nc, ident[:])
         ag_sb = keep.tile([P, K], BF16, name="ag_sb")
@@ -73,13 +76,12 @@ def tile_phiaslossengine_pb_s_kernel(tc, ag_diff, tension, hiddens, W_io, w_it, 
 
         def load_vecs():
             q = nc.scalar if VEC_Q == "scalar" else nc.gpsimd if VEC_Q == "gpsimd" else nc.sync
+            q.dma_start(out=tens[0:1, :], in_=tension.rearrange("c o -> o c"))
             for v, vec in enumerate((w_it, b_ih, b_hh)):
                 q.dma_start(out=vecs[v * VEC_R : (v + 1) * VEC_R, :], in_=vec.rearrange("(a f) -> a f", a=VEC_R))
 
         nc.sync.dma_start(out=ag_sb[:], in_=ag_diff)
         nc.sync.dma_start(out=h_sb[:], in_=hiddens)
-        if TENS_AT == -1:
-            nc.sync.dma_start(out=tens[:], in_=tension.rearrange("c o -> (c o)").partition_broadcast(P))
         if VEC_AT == -1:
             load_vecs()
         for i, unit in enumerate(units):
@@ -90,8 +92,6 @@ def tile_phiaslossengine_pb_s_kernel(tc, ag_diff, tension, hiddens, W_io, w_it, 
                 out=w_sb[unit][:],
                 in_=(W_io, W_hh)[m][first : first + HALF, :].rearrange("(p e) k -> p (e k)", e=E),
             )
-            if i == TENS_AT:
-                nc.sync.dma_start(out=tens[:], in_=tension.rearrange("c o -> (c o)").partition_broadcast(P))
             if i == VEC_AT:
                 load_vecs()
         nc.scalar.activation(out=warm[:], in_=warm[:], func=ACT.Sigmoid)
@@ -134,15 +134,19 @@ def tile_phiaslossengine_pb_s_kernel(tc, ag_diff, tension, hiddens, W_io, w_it, 
             quantised[key] = (codes, scales)
 
         def vectors_pe():
-            ps = acc_pool.tile([P, VEC_W, P], F32, tag="acc")
+            ps = acc_pool.tile([P, VEC_W + 1, P], F32, tag="acc")
             cols["ps"] = ps
+            nc.tensor.matmul(out=ps[:, VEC_W, :], lhsT=ones[:], rhs=tens[:], start=True, stop=True)
             for j in range(VEC_W):
                 nc.tensor.transpose(ps[:, j, :], vecs[:, j * HALF : (j + 1) * HALF].bitcast(F32), ident[:])
 
         def vectors_v():
             wide = VEC_R * E
             cols_all = keep.tile([P, VEC_W, 3 * wide], F32, name="cols_all")
-            nc.vector.tensor_copy(out=cols_all[:], in_=cols["ps"][:].bitcast(BF16)[:, :, 0 : 3 * wide])
+            nc.vector.tensor_copy(out=cols_all[:], in_=cols["ps"][:].bitcast(BF16)[:, 0:VEC_W, 0 : 3 * wide])
+            tension_rows = keep.tile([P, CELLS], F32, name="tension_rows")
+            nc.vector.tensor_copy(out=tension_rows[:], in_=cols["ps"][:, VEC_W, :])
+            cols["tension"] = tension_rows[:]
             b_sum = keep.tile([P, VEC_W, wide], F32, name="b_sum")
             nc.vector.tensor_add(out=b_sum[:], in0=cols_all[:, :, wide : 2 * wide], in1=cols_all[:, :, 2 * wide : 3 * wide])
             cols["w_it"] = cols_all[:, :, 0:wide]
@@ -187,7 +191,7 @@ def tile_phiaslossengine_pb_s_kernel(tc, ag_diff, tension, hiddens, W_io, w_it, 
             for e in range(E):
                 nc.vector.scalar_tensor_tensor(
                     out=p[:, e, :],
-                    in0=tens[:],
+                    in0=cols["tension"],
                     scalar=col("w_it", half, gate, e),
                     in1=acc[(half, gate)][:, 0, e, :],
                     op0=MULT,

@@ -28,21 +28,22 @@ MEAN_OVER_KEPT = (1.0 - KEEP) / (FACTION * KEEP)
 VEC_ROWS = 2
 VEC_HALVES = 3
 
-FLIP_BANKS = 4
-ACC_BANKS = 4
-SEQG = ((0, 0), (2, 0), (0, 1), (2, 1), (1, 0), (1, 1))
-RUNS = (1, 1, 1, 1, 1, 1)
+FLIP_BANKS = 5
+ACC_BANKS = 3
+SEQG = ((0, 0), (0, 1), (2, 0), (1, 0), (2, 1), (1, 1))
+RUNS = (2, 1, 1, 1, 1)
 TENS_AT = 2
 VEC_R = 2
 VEC_W = 3
-VPE = 4
-VV = 5
+VPE = 1
+VV = 2
 VEC_Q = "sync"
-VEC_AT = 4
+VEC_AT = 2
 V_COPIES = (1, 4)
 OUT_ENG = "S"
 BACK_ENG = {"n": "S", "moved": "S"}
-LAG = {"quant": 2, "mult": 6, "pre": 7, "rh": 7, "add": 8, "act": 7, "actn": 8, "diff": 11, "mul": 9, "zadd": 11, "zsum": 11, "zblend": 11, "turn": 11, "out": 11}
+THIN = ((1, 1), (1, 2), (0, 2))
+LAG = {"quant": 2, "mult": 4, "pre": 4, "rh": 4, "add": 5, "act": 4, "actn": 5, "diff": 7, "mul": 6, "zadd": 7, "zsum": 9, "zblend": 10, "turn": 10, "out": 10}
 SEQ = ("mult", "pre", "rh", "add", "act", "actn", "diff", "mul", "zadd", "zsum", "zblend", "turn", "out")
 MEAN = 0.15 / 16
 FLOPS = 2 * 2 * CELLS * K * 3 * HID
@@ -159,6 +160,9 @@ def tile_phiaslossengine_pb_s_kernel(tc, ag_diff, tension, hiddens, W_io, w_it, 
             at = row * E + e
             return cols[name][:, j, at : at + 1]
 
+        def spans(half, gate):
+            return (slice(0, 1), slice(1, 2)) if (half, gate) in THIN else (slice(0, E),)
+
         def mx_pass(acc_block, half, gate, m, e, start, stop):
             codes, scales = quantised[(half, gate, m)]
             codes_x, scales_x = quantised["x"]
@@ -211,9 +215,9 @@ def tile_phiaslossengine_pb_s_kernel(tc, ag_diff, tension, hiddens, W_io, w_it, 
                 )
 
         def n_add(half):
-            for e in range(E):
-                p = pre[(half, GATE_N)]
-                nc.vector.tensor_add(out=p[:, e, :], in0=p[:, e, :], in1=rh[half][:, e, :])
+            p = pre[(half, GATE_N)]
+            for s in spans(half, GATE_N):
+                nc.vector.tensor_add(out=p[:, s, :], in0=p[:, s, :], in1=rh[half][:, s, :])
 
         def gate_act(half, gate):
             result = half_tile("gate%d" % gate, half)
@@ -233,32 +237,37 @@ def tile_phiaslossengine_pb_s_kernel(tc, ag_diff, tension, hiddens, W_io, w_it, 
 
         def z_mul(half):
             moved[half] = half_tile("moved", half)
-            for e in range(E):
-                nc.vector.tensor_mul(out=moved[half][:, e, :], in0=gate_out[(half, GATE_Z)][:, e, :], in1=diff[half][:, e, :])
+            for s in spans(half, GATE_Z):
+                nc.vector.tensor_mul(out=moved[half][:, s, :], in0=gate_out[(half, GATE_Z)][:, s, :], in1=diff[half][:, s, :])
 
-        by_faction = "p (f s) -> p f s"
+        by_faction = "p e (f s) -> p (e f) s"
         n_sums = CELLS // FACTION
 
         def z_add(half):
             new[half] = half_tile("new", half)
-            for e in range(E):
-                nc.vector.tensor_add(out=new[half][:, e, :], in0=gate_out[(half, GATE_N)][:, e, :], in1=moved[half][:, e, :])
+            for s in spans(half, GATE_Z):
+                nc.vector.tensor_add(out=new[half][:, s, :], in0=gate_out[(half, GATE_N)][:, s, :], in1=moved[half][:, s, :])
 
         def z_sum(half):
-            sums[half] = keep.tile([P, E, n_sums], F32, name="sums_%d" % half)
-            for e in range(E):
+            sums_tile = keep.tile([P, E, n_sums], F32, name="sums_%d" % half)
+            sums[half] = sums_tile
+            for s in spans(half, GATE_Z):
                 nc.vector.tensor_reduce(
-                    out=sums[half][:, e, :], in_=new[half][:, e, :].rearrange(by_faction, s=FACTION), axis=mybir.AxisListType.X, op=ADD
+                    out=sums_tile[:, s, :].rearrange("p e f -> p (e f)"),
+                    in_=new[half][:, s, :].rearrange(by_faction, s=FACTION),
+                    axis=mybir.AxisListType.X,
+                    op=ADD,
                 )
 
         def z_blend(half):
             blend[half] = half_tile("blend", half)
-            for e in range(E):
+            for s in spans(half, GATE_Z):
+                flat = sums[half][:, s, :].rearrange("p e f -> p (e f)")
                 nc.vector.scalar_tensor_tensor(
-                    out=blend[half][:, e, :].rearrange(by_faction, s=FACTION),
-                    in0=sums[half][:, e, :].unsqueeze(2).to_broadcast([P, n_sums, FACTION]),
+                    out=blend[half][:, s, :].rearrange(by_faction, s=FACTION),
+                    in0=flat.unsqueeze(2).to_broadcast([P, (s.stop - s.start) * n_sums, FACTION]),
                     scalar=MEAN_OVER_KEPT,
-                    in1=new[half][:, e, :].rearrange(by_faction, s=FACTION),
+                    in1=new[half][:, s, :].rearrange(by_faction, s=FACTION),
                     op0=MULT,
                     op1=ADD,
                 )

@@ -28,23 +28,23 @@ MEAN_OVER_KEPT = (1.0 - KEEP) / (FACTION * KEEP)
 VEC_ROWS = 2
 VEC_HALVES = 3
 
-FLIP_BANKS = 5
-ACC_BANKS = 3
-SEQG = ((0, 0), (0, 1), (2, 0), (1, 0), (2, 1), (1, 1))
-RUNS = (2, 1, 1, 1, 1)
+FLIP_BANKS = 4
+ACC_BANKS = 4
+SEQG = ((0, 0), (2, 0), (0, 1), (1, 0), (2, 1), (1, 1))
+RUNS = (1,2,1,1,1)
 TENS_AT = 2
 VEC_R = 2
 VEC_W = 3
-VPE = 1
-VV = 2
+VPE = 2
+VV = 4
 VEC_Q = "sync"
 VEC_AT = 2
-V_COPIES = (1, 4)
+V_COPIES = (0,)
 OUT_ENG = "S"
-BACK_ENG = {"n": "S", "moved": "S"}
-THIN = ((1, 1), (1, 2), (0, 2))
-LAG = {"quant": 2, "mult": 4, "pre": 4, "rh": 4, "add": 5, "act": 4, "actn": 5, "diff": 7, "mul": 6, "zadd": 7, "zsum": 9, "zblend": 10, "turn": 10, "out": 10}
-SEQ = ("mult", "pre", "rh", "add", "act", "actn", "diff", "mul", "zadd", "zsum", "zblend", "turn", "out")
+BACK_ENG = {"n": "S", "moved": "S", "new": "S"}
+LAG = {"quant": 4, "mult": 4, "pre": 7, "rh": 7, "add": 8, "act": 8, "actn": 9, "diff": 11, "mul": 10, "zadd": 10, "zsum": 11, "zblend": 12, "turn": 12, "out": 12, "npe": 9, "ncopy": 10, "mixn": 12, "mpe": 12, "mcopy": 12, "mix": 12}
+SEQ = ("mult", "pre", "rh", "add", "act", "actn", "diff", "npe", "ncopy", "mixn", "mul", "zadd", "zsum", "zblend", "turn", "mpe", "mcopy", "mix", "out")
+MODE = (2, 0)
 MEAN = 0.15 / 16
 FLOPS = 2 * 2 * CELLS * K * 3 * HID
 
@@ -70,6 +70,7 @@ def tile_phiaslossengine_pb_s_kernel(tc, ag_diff, tension, hiddens, W_io, w_it, 
         nc.vector.memset(ones[:], 1.0)
         ident = keep.tile([P, P], F32, name="ident")
         make_identity(nc, ident[:])
+
         ag_sb = keep.tile([P, K], BF16, name="ag_sb")
         h_sb = keep.tile([P, K], BF16, name="h_sb")
         units = [(half, gate, m) for gate, half in SEQG for m in range(2)]
@@ -96,6 +97,23 @@ def tile_phiaslossengine_pb_s_kernel(tc, ag_diff, tension, hiddens, W_io, w_it, 
             if i == VEC_AT:
                 load_vecs()
         nc.scalar.activation(out=warm[:], in_=warm[:], func=ACT.Sigmoid)
+        factions = keep.tile([P, P], F32, name="factions")
+        nc.gpsimd.memset(factions[:], 0.0)
+        same_faction = [[-FACTION, P // FACTION], [0, FACTION]]
+        nc.gpsimd.affine_select(
+            out=factions[:], in_=factions[:], compare_op=mybir.AluOpType.is_gt, fill=1.0,
+            base=1 - FACTION, pattern=same_faction, channel_multiplier=1,
+        )
+        nc.gpsimd.affine_select(
+            out=factions[:], in_=factions[:], compare_op=mybir.AluOpType.is_ge, fill=0.0,
+            base=0, pattern=same_faction, channel_multiplier=1,
+        )
+        mean_sb = keep.tile([P, P], F32, name="mean_sb")
+        nc.gpsimd.tensor_scalar(out=mean_sb[:], in0=factions[:], scalar1=MEAN, scalar2=0.0, op0=MULT, op1=ADD)
+        keep_sb = keep.tile([P, P], F32, name="keep_sb")
+        nc.gpsimd.tensor_scalar(out=keep_sb[:], in0=ident[:], scalar1=KEEP, scalar2=0.0, op0=MULT, op1=ADD)
+        blend_sb = keep.tile([P, P], F32, name="blend_sb")
+        nc.gpsimd.tensor_add(out=blend_sb[:], in0=mean_sb[:], in1=keep_sb[:])
 
         banks = {}
         grouped = {}
@@ -107,6 +125,8 @@ def tile_phiaslossengine_pb_s_kernel(tc, ag_diff, tension, hiddens, W_io, w_it, 
         cols = {}
         moved = {}
         new = {}
+        back = {}
+        back_ps = {}
         blend = {}
         sums = {}
         rh = {}
@@ -160,9 +180,6 @@ def tile_phiaslossengine_pb_s_kernel(tc, ag_diff, tension, hiddens, W_io, w_it, 
             at = row * E + e
             return cols[name][:, j, at : at + 1]
 
-        def spans(half, gate):
-            return (slice(0, 1), slice(1, 2)) if (half, gate) in THIN else (slice(0, E),)
-
         def mx_pass(acc_block, half, gate, m, e, start, stop):
             codes, scales = quantised[(half, gate, m)]
             codes_x, scales_x = quantised["x"]
@@ -215,9 +232,9 @@ def tile_phiaslossengine_pb_s_kernel(tc, ag_diff, tension, hiddens, W_io, w_it, 
                 )
 
         def n_add(half):
-            p = pre[(half, GATE_N)]
-            for s in spans(half, GATE_N):
-                nc.vector.tensor_add(out=p[:, s, :], in0=p[:, s, :], in1=rh[half][:, s, :])
+            for e in range(E):
+                p = pre[(half, GATE_N)]
+                nc.vector.tensor_add(out=p[:, e, :], in0=p[:, e, :], in1=rh[half][:, e, :])
 
         def gate_act(half, gate):
             result = half_tile("gate%d" % gate, half)
@@ -237,40 +254,67 @@ def tile_phiaslossengine_pb_s_kernel(tc, ag_diff, tension, hiddens, W_io, w_it, 
 
         def z_mul(half):
             moved[half] = half_tile("moved", half)
-            for s in spans(half, GATE_Z):
-                nc.vector.tensor_mul(out=moved[half][:, s, :], in0=gate_out[(half, GATE_Z)][:, s, :], in1=diff[half][:, s, :])
+            for e in range(E):
+                nc.vector.tensor_mul(out=moved[half][:, e, :], in0=gate_out[(half, GATE_Z)][:, e, :], in1=diff[half][:, e, :])
 
-        by_faction = "p e (f s) -> p (e f) s"
+        by_faction = "p (f s) -> p f s"
         n_sums = CELLS // FACTION
 
         def z_add(half):
             new[half] = half_tile("new", half)
-            for s in spans(half, GATE_Z):
-                nc.vector.tensor_add(out=new[half][:, s, :], in0=gate_out[(half, GATE_N)][:, s, :], in1=moved[half][:, s, :])
+            for e in range(E):
+                nc.vector.tensor_add(out=new[half][:, e, :], in0=gate_out[(half, GATE_N)][:, e, :], in1=moved[half][:, e, :])
 
         def z_sum(half):
-            sums_tile = keep.tile([P, E, n_sums], F32, name="sums_%d" % half)
-            sums[half] = sums_tile
-            for s in spans(half, GATE_Z):
+            sums[half] = keep.tile([P, E, n_sums], F32, name="sums_%d" % half)
+            for e in range(E):
                 nc.vector.tensor_reduce(
-                    out=sums_tile[:, s, :].rearrange("p e f -> p (e f)"),
-                    in_=new[half][:, s, :].rearrange(by_faction, s=FACTION),
-                    axis=mybir.AxisListType.X,
-                    op=ADD,
+                    out=sums[half][:, e, :], in_=new[half][:, e, :].rearrange(by_faction, s=FACTION), axis=mybir.AxisListType.X, op=ADD
                 )
 
         def z_blend(half):
             blend[half] = half_tile("blend", half)
-            for s in spans(half, GATE_Z):
-                flat = sums[half][:, s, :].rearrange("p e f -> p (e f)")
+            for e in range(E):
                 nc.vector.scalar_tensor_tensor(
-                    out=blend[half][:, s, :].rearrange(by_faction, s=FACTION),
-                    in0=flat.unsqueeze(2).to_broadcast([P, (s.stop - s.start) * n_sums, FACTION]),
+                    out=blend[half][:, e, :].rearrange(by_faction, s=FACTION),
+                    in0=sums[half][:, e, :].unsqueeze(2).to_broadcast([P, n_sums, FACTION]),
                     scalar=MEAN_OVER_KEPT,
-                    in1=new[half][:, s, :].rearrange(by_faction, s=FACTION),
+                    in1=new[half][:, e, :].rearrange(by_faction, s=FACTION),
                     op0=MULT,
                     op1=ADD,
                 )
+
+        def back_pe(half, name):
+            source = {"n": gate_out.get((half, GATE_N)), "moved": moved.get(half), "new": new.get(half)}[name]
+            ps = acc_pool.tile([P, E, P], F32, tag="acc")
+            back_ps[(name, half)] = ps
+            for e in range(E):
+                nc.tensor.transpose(ps[:, e, :], source[:, e, :], ident[:])
+
+        def back_copy(half, name):
+            t = half_tile("back_" + name, half)
+            back[(name, half)] = t
+            for e in range(E):
+                if BACK_ENG[name] == "S":
+                    nc.scalar.copy(out=t[:, e, :], in_=back_ps[(name, half)][:, e, :])
+                else:
+                    nc.vector.tensor_copy(out=t[:, e, :], in_=back_ps[(name, half)][:, e, :])
+
+        def flat(tile):
+            return tile[:].rearrange("c e p -> c (e p)")
+
+        def mix_n(half):
+            mixed = acc_pool.tile([P, E, P], F32, tag="acc")
+            out_ps[half] = mixed
+            nc.tensor.matmul(out=flat(mixed), lhsT=blend_sb[:], rhs=flat(back[("n", half)]), start=True, stop=False)
+
+        def mix(half):
+            if MODE[half] == 1:
+                mixed = acc_pool.tile([P, E, P], F32, tag="acc")
+                out_ps[half] = mixed
+                nc.tensor.matmul(out=flat(mixed), lhsT=blend_sb[:], rhs=flat(back[("new", half)]), start=True, stop=True)
+            else:
+                nc.tensor.matmul(out=flat(out_ps[half]), lhsT=blend_sb[:], rhs=flat(back[("moved", half)]), start=False, stop=True)
 
         def turn_out(half):
             turned = acc_pool.tile([P, E, P], F32, tag="acc")
@@ -281,8 +325,10 @@ def tile_phiaslossengine_pb_s_kernel(tc, ag_diff, tension, hiddens, W_io, w_it, 
         def out_half(half):
             out_sb = keep.tile([P, HALF], F32, name="out_sb_%d" % half)
             o = out_sb[:].rearrange("c (p e) -> c p e", e=E)
-            i = out_ps[half][:].rearrange("c e p -> c p e")
-            nc.scalar.activation(out=o, in_=i, func=ACT.Copy, scale=KEEP)
+            if MODE[half] == 0:
+                nc.scalar.activation(out=o, in_=out_ps[half][:].rearrange("c e p -> c p e"), func=ACT.Copy, scale=KEEP)
+            else:
+                nc.scalar.copy(out=o, in_=out_ps[half][:].rearrange("c e p -> c p e"))
             nc.sync.dma_start(out=out[:, half * HALF : (half + 1) * HALF], in_=out_sb[:])
 
         turn("x", ag_sb[:].bitcast(F32), h_sb[:].bitcast(F32))
@@ -326,13 +372,25 @@ def tile_phiaslossengine_pb_s_kernel(tc, ag_diff, tension, hiddens, W_io, w_it, 
                         make_diff(half)
                     elif stage == "mul" and gate == GATE_Z:
                         z_mul(half)
-                    elif stage == "zadd" and gate == GATE_Z:
+                    elif stage == "npe" and gate == GATE_N and MODE[half] == 2:
+                        back_pe(half, "n")
+                    elif stage == "ncopy" and gate == GATE_N and MODE[half] == 2:
+                        back_copy(half, "n")
+                    elif stage == "mixn" and gate == GATE_N and MODE[half] == 2:
+                        mix_n(half)
+                    elif stage == "mpe" and gate == GATE_Z and MODE[half]:
+                        back_pe(half, "moved" if MODE[half] == 2 else "new")
+                    elif stage == "mcopy" and gate == GATE_Z and MODE[half]:
+                        back_copy(half, "moved" if MODE[half] == 2 else "new")
+                    elif stage == "mix" and gate == GATE_Z and MODE[half]:
+                        mix(half)
+                    elif stage == "zadd" and gate == GATE_Z and MODE[half] < 2:
                         z_add(half)
-                    elif stage == "zsum" and gate == GATE_Z:
+                    elif stage == "zsum" and gate == GATE_Z and MODE[half] == 0:
                         z_sum(half)
-                    elif stage == "zblend" and gate == GATE_Z:
+                    elif stage == "zblend" and gate == GATE_Z and MODE[half] == 0:
                         z_blend(half)
-                    elif stage == "turn" and gate == GATE_Z:
+                    elif stage == "turn" and gate == GATE_Z and MODE[half] == 0:
                         turn_out(half)
                     elif stage == "out" and gate == GATE_Z:
                         out_half(half)

from contextlib import ExitStack

import concourse.mybir as mybir
from concourse.masks import make_identity

F32 = mybir.dt.float32
BF16 = mybir.dt.bfloat16
U32 = mybir.dt.uint32
U8 = mybir.dt.uint8
FP8X4 = mybir.dt.float8_e4m3fn_x4
ADD = mybir.AluOpType.add
MULT = mybir.AluOpType.mult
ACT = mybir.ActivationFunctionType

P = 128
CELLS = 128
K = 512
HID = 512
WORDS = K // 2
E = 2
HALVES = 2
HALF = HID // HALVES
GATE_R, GATE_Z, GATE_N = 0, 1, 2
GATE_ORDER = (GATE_R, GATE_N, GATE_Z)
FACTION = 16
KEEP = 0.85
MEAN_OVER_KEPT = (1.0 - KEEP) / (FACTION * KEEP)
VEC_ROWS = 2
VEC_HALVES = 3

FLIP_BANKS = 4
ACC_BANKS = 4
SEQG = ((0, 0), (2, 0), (0, 1), (1, 0), (2, 1), (1, 1))
RUNS = (1,2,1,1,1)
TENS_AT = 2
VEC_R = 2
VEC_W = 3
VPE = 2
VV = 4
VEC_Q = "sync"
VEC_AT = 2
V_COPIES = (0,)
OUT_ENG = "S"
BACK_ENG = {"n": "S", "moved": "S", "new": "S"}
LAG = {"quant": 4, "mult": 4, "pre": 7, "rh": 7, "add": 8, "act": 8, "actn": 9, "diff": 11, "mul": 10, "zadd": 10, "zsum": 11, "zblend": 12, "turn": 12, "out": 12, "npe": 9, "ncopy": 10, "mixn": 12, "mpe": 12, "mcopy": 12, "mix": 12}
SEQ = ("mult", "pre", "rh", "add", "act", "actn", "diff", "npe", "ncopy", "mixn", "mul", "zadd", "zsum", "zblend", "turn", "mpe", "mcopy", "mix", "out")
MODE = (2, 0)
MEAN = 0.15 / 16
FLOPS = 2 * 2 * CELLS * K * 3 * HID


def tile_phiaslossengine_pb_s_kernel(tc, ag_diff, tension, hiddens, W_io, w_it, W_hh, b_ih, b_hh, out):
    nc = tc.nc
    with ExitStack() as stack:
        keep = stack.enter_context(tc.tile_pool(name="keep", bufs=1))
        flip_pool = stack.enter_context(tc.psum_pool(name="flip", bufs=FLIP_BANKS))
        acc_pool = stack.enter_context(tc.psum_pool(name="acc", bufs=ACC_BANKS))
        stack.enter_context(tc.manual_schedule())

        def half_tile(name, half):
            return keep.tile([P, E, CELLS], F32, name="%s_%d" % (name, half))

        vecs = keep.tile([P, VEC_W * HALF], BF16, name="vecs")
        tens = keep.tile([P, CELLS], BF16, name="tens")
        warm = keep.tile([P, 1], F32, name="warm")
        nc.vector.memset(warm[:], 0.0)
        nc.vector.memset(tens[:], 0.0)
        nc.vector.memset(vecs[:], 0.0)
        ones = keep.tile([P, P], BF16, name="ones")
        nc.vector.memset(ones[:], 1.0)
        ident = keep.tile([P, P], F32, name="ident")
        make_identity(nc, ident[:])

        ag_sb = keep.tile([P, K], BF16, name="ag_sb")
        h_sb = keep.tile([P, K], BF16, name="h_sb")
        units = [(half, gate, m) for gate, half in SEQG for m in range(2)]
        w_sb = {}

        def load_vecs():
            q = nc.scalar if VEC_Q == "scalar" else nc.gpsimd if VEC_Q == "gpsimd" else nc.sync
            q.dma_start(out=tens[0:1, :], in_=tension.rearrange("c o -> o c"))
            for v, vec in enumerate((w_it, b_ih, b_hh)):
                q.dma_start(out=vecs[v * VEC_R : (v + 1) * VEC_R, :], in_=vec.rearrange("(a f) -> a f", a=VEC_R))

        nc.sync.dma_start(out=ag_sb[:], in_=ag_diff)
        nc.sync.dma_start(out=h_sb[:], in_=hiddens)
        if VEC_AT == -1:
            load_vecs()
        for i, unit in enumerate(units):
            half, gate, m = unit
            first = gate * HID + half * HALF
            w_sb[unit] = keep.tile([P, E * K], BF16, name="w_%d_%d_%d" % unit)
            nc.sync.dma_start(
                out=w_sb[unit][:],
                in_=(W_io, W_hh)[m][first : first + HALF, :].rearrange("(p e) k -> p (e k)", e=E),
            )
            if i == VEC_AT:
                load_vecs()
        nc.scalar.activation(out=warm[:], in_=warm[:], func=ACT.Sigmoid)
        factions = keep.tile([P, P], F32, name="factions")
        nc.gpsimd.memset(factions[:], 0.0)
        same_faction = [[-FACTION, P // FACTION], [0, FACTION]]
        nc.gpsimd.affine_select(
            out=factions[:], in_=factions[:], compare_op=mybir.AluOpType.is_gt, fill=1.0,
            base=1 - FACTION, pattern=same_faction, channel_multiplier=1,
        )
        nc.gpsimd.affine_select(
            out=factions[:], in_=factions[:], compare_op=mybir.AluOpType.is_ge, fill=0.0,
            base=0, pattern=same_faction, channel_multiplier=1,
        )
        mean_sb = keep.tile([P, P], F32, name="mean_sb")
        nc.gpsimd.tensor_scalar(out=mean_sb[:], in0=factions[:], scalar1=MEAN, scalar2=0.0, op0=MULT, op1=ADD)
        keep_sb = keep.tile([P, P], F32, name="keep_sb")
        nc.gpsimd.tensor_scalar(out=keep_sb[:], in0=ident[:], scalar1=KEEP, scalar2=0.0, op0=MULT, op1=ADD)
        blend_sb = keep.tile([P, P], F32, name="blend_sb")
        nc.gpsimd.tensor_add(out=blend_sb[:], in0=mean_sb[:], in1=keep_sb[:])

        banks = {}
        grouped = {}
        quantised = {}
        acc = {}
        gate_out = {}
        pre = {}
        diff = {}
        cols = {}
        moved = {}
        new = {}
        back = {}
        back_ps = {}
        blend = {}
        sums = {}
        rh = {}
        out_ps = {}

        def turn(key, first_words, second_words):
            bank = flip_pool.tile([P, 2, 2, P], F32, tag="flip")
            banks[key] = bank
            for b, words in enumerate((first_words, second_words)):
                for u in range(2):
                    nc.tensor.transpose(banks[key][:, b, u, :], words[:, u * P : (u + 1) * P], ident[:])

        def copy(key, engine):
            grouped[key] = keep.tile([P, 2 * P * 4], BF16, name="grouped_%s" % str(key), align_bytes=64)
            o = grouped[key][:].bitcast(F32).rearrange("p (b c u) -> p b c u", b=2, u=2)
            i = banks[key][:].rearrange("p b u c -> p b c u")
            if engine == "S":
                nc.scalar.copy(out=o, in_=i)
            else:
                nc.vector.tensor_copy(out=o, in_=i)

        def quantise(key):
            codes = keep.tile([P, 2 * P], U32, name="codes_%s" % str(key), align_bytes=64)
            scales = keep.tile([P, 2 * P], U8, name="scales_%s" % str(key), align_bytes=64)
            nc.vector.quantize_mx(out=codes[:].bitcast(FP8X4), scales=scales[:], in_=grouped[key][:])
            quantised[key] = (codes, scales)

        def vectors_pe():
            ps = acc_pool.tile([P, VEC_W + 1, P], F32, tag="acc")
            cols["ps"] = ps
            nc.tensor.matmul(out=ps[:, VEC_W, :], lhsT=ones[:], rhs=tens[:], start=True, stop=True)
            for j in range(VEC_W):
                nc.tensor.transpose(ps[:, j, :], vecs[:, j * HALF : (j + 1) * HALF].bitcast(F32), ident[:])

        def vectors_v():
            wide = VEC_R * E
            cols_all = keep.tile([P, VEC_W, 3 * wide], F32, name="cols_all")
            nc.vector.tensor_copy(out=cols_all[:], in_=cols["ps"][:].bitcast(BF16)[:, 0:VEC_W, 0 : 3 * wide])
            tension_rows = keep.tile([P, CELLS], F32, name="tension_rows")
            nc.vector.tensor_copy(out=tension_rows[:], in_=cols["ps"][:, VEC_W, :])
            cols["tension"] = tension_rows[:]
            b_sum = keep.tile([P, VEC_W, wide], F32, name="b_sum")
            nc.vector.tensor_add(out=b_sum[:], in0=cols_all[:, :, wide : 2 * wide], in1=cols_all[:, :, 2 * wide : 3 * wide])
            cols["w_it"] = cols_all[:, :, 0:wide]
            cols["b_ih"] = cols_all[:, :, wide : 2 * wide]
            cols["b_hh"] = cols_all[:, :, 2 * wide : 3 * wide]
            cols["b_sum"] = b_sum[:]

        def col(name, half, gate, e):
            row, j = divmod(gate * HALVES + half, VEC_W)
            at = row * E + e
            return cols[name][:, j, at : at + 1]

        def mx_pass(acc_block, half, gate, m, e, start, stop):
            codes, scales = quantised[(half, gate, m)]
            codes_x, scales_x = quantised["x"]
            w_cols = slice(e * P, (e + 1) * P)
            x_cols = slice(m * CELLS, (m + 1) * CELLS)
            nc.tensor.matmul_mx(
                out=acc_block,
                lhsT=codes[:, w_cols].bitcast(FP8X4),
                lhsT_scale=scales[:, w_cols],
                rhs=codes_x[:, x_cols].bitcast(FP8X4),
                rhs_scale=scales_x[:, x_cols],
                start=start,
                stop=stop,
            )

        def multiply(half, gate):
            acc_tile = acc_pool.tile([P, 2, E, CELLS], F32, tag="acc")
            acc[(half, gate)] = acc_tile
            for e in range(E):
                if gate == GATE_N:
                    for m in range(2):
                        mx_pass(acc_tile[:, m, e, :], half, gate, m, e, True, True)
                else:
                    mx_pass(acc_tile[:, 0, e, :], half, gate, 0, e, True, False)
                    mx_pass(acc_tile[:, 0, e, :], half, gate, 1, e, False, True)

        def gate_pre(half, gate):
            p = half_tile("pre%d" % gate, half)
            pre[(half, gate)] = p
            for e in range(E):
                nc.vector.scalar_tensor_tensor(
                    out=p[:, e, :],
                    in0=cols["tension"],
                    scalar=col("w_it", half, gate, e),
                    in1=acc[(half, gate)][:, 0, e, :],
                    op0=MULT,
                    op1=ADD,
                )

        def n_rh(half):
            rh[half] = half_tile("rh", half)
            for e in range(E):
                nc.vector.scalar_tensor_tensor(
                    out=rh[half][:, e, :],
                    in0=acc[(half, GATE_N)][:, 1, e, :],
                    scalar=col("b_hh", half, GATE_N, e),
                    in1=gate_out[(half, GATE_R)][:, e, :],
                    op0=ADD,
                    op1=MULT,
                )

        def n_add(half):
            for e in range(E):
                p = pre[(half, GATE_N)]
                nc.vector.tensor_add(out=p[:, e, :], in0=p[:, e, :], in1=rh[half][:, e, :])

        def gate_act(half, gate):
            result = half_tile("gate%d" % gate, half)
            for e in range(E):
                nc.scalar.activation(
                    out=result[:, e, :],
                    in_=pre[(half, gate)][:, e, :],
                    func=ACT.Tanh if gate == GATE_N else ACT.Sigmoid,
                    bias=col("b_ih" if gate == GATE_N else "b_sum", half, gate, e),
                )
            gate_out[(half, gate)] = result

        def make_diff(half):
            h_turned = grouped["x"][:].rearrange("p (b c u e) -> p b u e c", b=2, u=2, e=2)
            diff[half] = half_tile("diff", half)
            nc.vector.tensor_sub(out=diff[half][:], in0=h_turned[:, 1, half, :, :], in1=gate_out[(half, GATE_N)][:])

        def z_mul(half):
            moved[half] = half_tile("moved", half)
            for e in range(E):
                nc.vector.tensor_mul(out=moved[half][:, e, :], in0=gate_out[(half, GATE_Z)][:, e, :], in1=diff[half][:, e, :])

        by_faction = "p (f s) -> p f s"
        n_sums = CELLS // FACTION

        def z_add(half):
            new[half] = half_tile("new", half)
            for e in range(E):
                nc.vector.tensor_add(out=new[half][:, e, :], in0=gate_out[(half, GATE_N)][:, e, :], in1=moved[half][:, e, :])

        def z_sum(half):
            sums[half] = keep.tile([P, E, n_sums], F32, name="sums_%d" % half)
            for e in range(E):
                nc.vector.tensor_reduce(
                    out=sums[half][:, e, :], in_=new[half][:, e, :].rearrange(by_faction, s=FACTION), axis=mybir.AxisListType.X, op=ADD
                )

        def z_blend(half):
            blend[half] = half_tile("blend", half)
            for e in range(E):
                nc.vector.scalar_tensor_tensor(
                    out=blend[half][:, e, :].rearrange(by_faction, s=FACTION),
                    in0=sums[half][:, e, :].unsqueeze(2).to_broadcast([P, n_sums, FACTION]),
                    scalar=MEAN_OVER_KEPT,
                    in1=new[half][:, e, :].rearrange(by_faction, s=FACTION),
                    op0=MULT,
                    op1=ADD,
                )

        def back_pe(half, name):
            source = {"n": gate_out.get((half, GATE_N)), "moved": moved.get(half), "new": new.get(half)}[name]
            ps = acc_pool.tile([P, E, P], F32, tag="acc")
            back_ps[(name, half)] = ps
            for e in range(E):
                nc.tensor.transpose(ps[:, e, :], source[:, e, :], ident[:])

        def back_copy(half, name):
            t = half_tile("back_" + name, half)
            back[(name, half)] = t
            for e in range(E):
                if BACK_ENG[name] == "S":
                    nc.scalar.copy(out=t[:, e, :], in_=back_ps[(name, half)][:, e, :])
                else:
                    nc.vector.tensor_copy(out=t[:, e, :], in_=back_ps[(name, half)][:, e, :])

        def flat(tile):
            return tile[:].rearrange("c e p -> c (e p)")

        def mix_n(half):
            mixed = acc_pool.tile([P, E, P], F32, tag="acc")
            out_ps[half] = mixed
            nc.tensor.matmul(out=flat(mixed), lhsT=blend_sb[:], rhs=flat(back[("n", half)]), start=True, stop=False)

        def mix(half):
            if MODE[half] == 1:
                mixed = acc_pool.tile([P, E, P], F32, tag="acc")
                out_ps[half] = mixed
                nc.tensor.matmul(out=flat(mixed), lhsT=blend_sb[:], rhs=flat(back[("new", half)]), start=True, stop=True)
            else:
                nc.tensor.matmul(out=flat(out_ps[half]), lhsT=blend_sb[:], rhs=flat(back[("moved", half)]), start=False, stop=True)

        def turn_out(half):
            turned = acc_pool.tile([P, E, P], F32, tag="acc")
            out_ps[half] = turned
            for e in range(E):
                nc.tensor.transpose(out_ps[half][:, e, :], blend[half][:, e, :], ident[:])

        def out_half(half):
            out_sb = keep.tile([P, HALF], F32, name="out_sb_%d" % half)
            o = out_sb[:].rearrange("c (p e) -> c p e", e=E)
            if MODE[half] == 0:
                nc.scalar.activation(out=o, in_=out_ps[half][:].rearrange("c e p -> c p e"), func=ACT.Copy, scale=KEEP)
            else:
                nc.scalar.copy(out=o, in_=out_ps[half][:].rearrange("c e p -> c p e"))
            nc.sync.dma_start(out=out[:, half * HALF : (half + 1) * HALF], in_=out_sb[:])

        turn("x", ag_sb[:].bitcast(F32), h_sb[:].bitcast(F32))
        copy("x", "S")
        n = len(units)
        groups = {}
        g = 0
        for size in RUNS:
            groups[2 * (g + size) - 1] = [(half, gate) for gate, half in SEQG[g : g + size]]
            g += size
        for tick in range(n + 20):
            if tick < n:
                words = w_sb[units[tick]][:].bitcast(F32)
                turn(units[tick], words[:, 0:WORDS], words[:, WORDS : 2 * WORDS])
            if tick < n:
                copy(units[tick], "V" if tick in V_COPIES else "S")
            if tick == VPE:
                vectors_pe()
            if tick == 0:
                quantise("x")
            if tick == VV:
                vectors_v()
            if 0 <= tick - LAG["quant"] < n:
                quantise(units[tick - LAG["quant"]])

            for stage in SEQ:
                for half, gate in groups.get(tick - LAG[stage], ()):
                    if stage == "mult":
                        multiply(half, gate)
                    elif stage == "pre":
                        gate_pre(half, gate)
                    elif stage == "rh" and gate == GATE_N:
                        n_rh(half)
                    elif stage == "add" and gate == GATE_N:
                        n_add(half)
                    elif stage == "act" and gate != GATE_N:
                        gate_act(half, gate)
                    elif stage == "actn" and gate == GATE_N:
                        gate_act(half, gate)
                    elif stage == "diff" and gate == GATE_N:
                        make_diff(half)
                    elif stage == "mul" and gate == GATE_Z:
                        z_mul(half)
                    elif stage == "npe" and gate == GATE_N and MODE[half] == 2:
                        back_pe(half, "n")
                    elif stage == "ncopy" and gate == GATE_N and MODE[half] == 2:
                        back_copy(half, "n")
                    elif stage == "mixn" and gate == GATE_N and MODE[half] == 2:
                        mix_n(half)
                    elif stage == "mpe" and gate == GATE_Z and MODE[half]:
                        back_pe(half, "moved" if MODE[half] == 2 else "new")
                    elif stage == "mcopy" and gate == GATE_Z and MODE[half]:
                        back_copy(half, "moved" if MODE[half] == 2 else "new")
                    elif stage == "mix" and gate == GATE_Z and MODE[half]:
                        mix(half)
                    elif stage == "zadd" and gate == GATE_Z and MODE[half] < 2:
                        z_add(half)
                    elif stage == "zsum" and gate == GATE_Z and MODE[half] == 0:
                        z_sum(half)
                    elif stage == "zblend" and gate == GATE_Z and MODE[half] == 0:
                        z_blend(half)
                    elif stage == "turn" and gate == GATE_Z and MODE[half] == 0:
                        turn_out(half)
                    elif stage == "out" and gate == GATE_Z:
                        out_half(half)
